import numpy as np
import ml_dtypes


def mxq(x, axis, fmt="e4m3"):
    dtype, down = {"e4m3": (ml_dtypes.float8_e4m3fn, 7), "e5m2": (ml_dtypes.float8_e5m2, 14)}[fmt]
    v = np.moveaxis(np.asarray(x, np.float32).astype(ml_dtypes.bfloat16).astype(np.float64), axis, -1)
    blocks = v.reshape(v.shape[:-1] + (-1, 32))
    amax = np.abs(blocks).max(-1, keepdims=True)
    byte = np.maximum(np.where(amax > 0, np.frexp(amax)[1] - 1 + 127, 0) - down, 1)
    scale = np.exp2(byte - 127.0)
    codes = (blocks / scale).astype(np.float32).astype(dtype).astype(np.float64)
    return np.moveaxis((codes * scale).reshape(v.shape), -1, axis)


WIDE = False


def mx_kscale(k):
    if not WIDE:
        return np.ones(k)
    levels = np.array([10, -10, 5, -5, 0])
    a = np.random.permutation(np.resize(levels, k // 512 * 4)).reshape(k // 512, 4)
    idx = np.arange(k)
    return np.exp2(a[idx // 512, idx % 128 // 32])


BF16 = ml_dtypes.bfloat16


def bf(x):
    return np.asarray(x, np.float32).astype(BF16)


def f64(x):
    return np.asarray(x).astype(np.float64)


B, CX, CT, N, T, C, K = 2, 512, 512, 2, 512, 1024, 8
CIN = CX + CT
DH = C // K
SMALL_VALUE = -32767.0


def heads(t):
    return t.reshape(B, K, DH, N, T).transpose(1, 0, 3, 4, 2)


def setup_inputs():
    s = mx_kscale(CIN)
    return {"x": bf(np.random.standard_normal((B, CX, N, T)) * s[:CX][None, :, None, None]),
            "tem_embedding": bf(np.random.standard_normal((B, CT, N, T)) * s[CX:][None, :, None, None]),
            "Wv": bf(np.random.standard_normal((C, CIN)) / np.sqrt(CIN) / s[None, :]),
            "bv": bf(np.random.standard_normal(C) * 0.1),
            "q": bf(np.random.standard_normal((B, C, N, T)) * 1.5),
            "k": bf(np.random.standard_normal((B, C, N, T)) * 1.5)}


def reference(x, tem_embedding, Wv, bv, q, k):
    xin = np.concatenate([f64(x), f64(tem_embedding)[:, :, :, -T:]], axis=1).reshape(B, CIN, N * T)
    v = ((mxq(f64(Wv), 1, "e4m3") @ mxq(xin, 1, "e4m3")) + f64(bv)[None, :, None]).reshape(B, C, N, T)
    qh, kh, vh = heads(f64(q)), heads(f64(k)), heads(v)
    scores = qh @ kh.transpose(0, 1, 2, 4, 3) / np.sqrt(DH)
    causal = np.tril(np.ones((T, T), dtype=bool))
    scores = np.where(causal, scores, SMALL_VALUE)
    e = np.exp(scores - scores.max(-1, keepdims=True))
    out = (mxq(e, 4, "e4m3") @ mxq(vh, 3, "e4m3")) / e.sum(-1, keepdims=True)
    return out.transpose(1, 0, 4, 2, 3).reshape(B, C, N, T)

@@ -1,0 +1,263 @@
+import math
+from contextlib import ExitStack
+
+import concourse.mybir as mybir
+from concourse.masks import make_identity
+
+F32 = mybir.dt.float32
+BF16 = mybir.dt.bfloat16
+U32 = mybir.dt.uint32
+U8 = mybir.dt.uint8
+FP8X4 = mybir.dt.float8_e4m3fn_x4
+ALU = mybir.AluOpType
+ACT = mybir.ActivationFunctionType
+
+P = 128
+PACK = 4
+B, NODES, T, HEADS, DH = 2, 2, 512, 8, 128
+CIN = 1024
+PASSES = CIN // (P * PACK)
+BLOCKS = T // P
+SCALE = 1.0 / math.sqrt(DH)
+MASK_ADDEND = -(2.0**19)
+
+FLOPS = 2 * B * NODES * T * CIN * HEADS * DH + 2 * (2 * B * NODES * HEADS * T * T * DH)
+
+
+def tile_tatt_pa_kernel(tc, x, tem_embedding, Wv, bv, q, k, out):
+    nc = tc.nc
+    heads = [(b, h, n) for b in range(B) for h in range(HEADS) for n in range(NODES)]
+
+    with ExitStack() as ctx:
+        keep = ctx.enter_context(tc.tile_pool(name="keep", bufs=1))
+        stage = ctx.enter_context(tc.tile_pool(name="stage", bufs=2))
+        rows = ctx.enter_context(tc.tile_pool(name="rows", bufs=2 * BLOCKS))
+        small = ctx.enter_context(tc.tile_pool(name="small", bufs=3))
+        handoff = ctx.enter_context(tc.tile_pool(name="handoff", bufs=3))
+        ps_scores = ctx.enter_context(tc.psum_pool(name="ps_scores", bufs=3))
+        ps_et = ctx.enter_context(tc.psum_pool(name="ps_et", bufs=2))
+        ps_misc = ctx.enter_context(tc.psum_pool(name="ps_misc", bufs=1))
+
+        q_all = keep.tile([P, B * HEADS, NODES * T], BF16)
+        k_all = keep.tile([P, B * HEADS, NODES * T], BF16)
+        wv_raw = keep.tile([P, HEADS, CIN], BF16)
+        xin_raw = keep.tile([P, B, PASSES, PACK, NODES * T], BF16)
+        bias_all = keep.tile([P, HEADS * DH], BF16)
+
+        def load_qk(b, h):
+            channels = slice(h * DH, (h + 1) * DH)
+            nc.sync.dma_start(out=q_all[:, b * HEADS + h, :], in_=q[b, channels].rearrange("c n t -> c (n t)"))
+            nc.sync.dma_start(out=k_all[:, b * HEADS + h, :], in_=k[b, channels].rearrange("c n t -> c (n t)"))
+
+        def load_xin(b):
+            for g, stream in enumerate((x, tem_embedding)):
+                nc.sync.dma_start(
+                    out=xin_raw[:, b, g], in_=stream[b].rearrange("(p j) n t -> p j (n t)", j=PACK)
+                )
+
+        nc.gpsimd.dma_start(out=bias_all[:], in_=bv.partition_broadcast(P))
+        load_qk(0, 0)
+        load_xin(0)
+        for h in range(HEADS):
+            nc.sync.dma_start(out=wv_raw[:, h, :], in_=Wv[h * DH : (h + 1) * DH, :])
+            if h > 0:
+                load_qk(0, h)
+        load_xin(1)
+        for h in range(HEADS):
+            load_qk(1, h)
+
+        ident_bf = keep.tile([P, P], BF16)
+        make_identity(nc, ident_bf[:])
+        ident_f32 = keep.tile([P, P], F32)
+        make_identity(nc, ident_f32[:])
+        mask_f32 = keep.tile([P, P], F32)
+        nc.gpsimd.memset(mask_f32[:], 0.0)
+        nc.gpsimd.affine_select(
+            out=mask_f32[:],
+            in_=mask_f32[:],
+            compare_op=ALU.is_ge,
+            fill=MASK_ADDEND,
+            base=0,
+            pattern=[[-1, P]],
+            channel_multiplier=1,
+        )
+        mask_bf = keep.tile([P, P], BF16)
+        nc.vector.tensor_copy(out=mask_bf[:], in_=mask_f32[:])
+
+        grouped_e = [
+            keep.tile([P, T, PACK], BF16, align_bytes=64, name="grouped_e%d" % r) for r in range(2)
+        ]
+        for tile_e in grouped_e:
+            nc.vector.memset(tile_e[:], 0.0)
+
+        x_codes = keep.tile([P, B, PASSES, NODES * T], U32, align_bytes=64)
+        x_scales = keep.tile([P, B, PASSES, NODES * T], U8, align_bytes=64)
+        w_codes = keep.tile([P, HEADS, PASSES, DH], U32, align_bytes=64)
+        w_scales = keep.tile([P, HEADS, PASSES, DH], U8, align_bytes=64)
+
+        def quantise_xin(b, n):
+            steps = slice(n * T, (n + 1) * T)
+            for g in range(PASSES):
+                x_grouped = stage.tile([P, T, PACK], BF16, align_bytes=64)
+                nc.vector.tensor_copy(
+                    out=x_grouped[:].rearrange("p (c i) j -> p c j i", i=4),
+                    in_=xin_raw[:, b, g, :, steps].rearrange("p j (c i) -> p c j i", i=4),
+                )
+                nc.vector.quantize_mx(
+                    out=x_codes[:, b, g, steps].bitcast(FP8X4),
+                    scales=x_scales[:, b, g, steps],
+                    in_=x_grouped[:].rearrange("p t j -> p (t j)"),
+                )
+
+        def quantise_wv(h):
+            words = wv_raw[:, h, :].bitcast(F32)
+            words_per_pass = P * PACK // 2
+            wt_ps = ps_misc.tile([P, PASSES, 2, DH], F32, tag="r")
+            for g in range(PASSES):
+                for half in range(2):
+                    nc.tensor.transpose(
+                        wt_ps[:, g, half, :],
+                        words[:, g * words_per_pass + half : (g + 1) * words_per_pass : 2],
+                        ident_f32[:],
+                    )
+            w_grouped = stage.tile([P, PASSES * DH * PACK], BF16, align_bytes=64)
+            nc.scalar.copy(
+                out=w_grouped[:].bitcast(F32).rearrange("p (g o half) -> p g o half", g=PASSES, half=2),
+                in_=wt_ps[:].rearrange("p g half o -> p g o half"),
+            )
+            nc.vector.quantize_mx(
+                out=w_codes[:, h].rearrange("p g o -> p (g o)").bitcast(FP8X4),
+                scales=w_scales[:, h].rearrange("p g o -> p (g o)"),
+                in_=w_grouped[:],
+            )
+
+        def softmax_rows(head):
+            b, h, n = head
+            q_head = q_all[:, b * HEADS + h, n * T : (n + 1) * T]
+            k_head = k_all[:, b * HEADS + h, n * T : (n + 1) * T]
+            shift = small.tile([P, BLOCKS], F32)
+            rowsum = small.tile([P, BLOCKS], F32)
+            e_rows = []
+            for i in range(BLOCKS):
+                width = (i + 1) * P
+                s_ps = ps_scores.tile([P, T], F32)
+                nc.tensor.matmul(
+                    out=s_ps[:, 0:width],
+                    lhsT=q_head[:, i * P : (i + 1) * P],
+                    rhs=k_head[:, 0:width],
+                    start=True,
+                    stop=False,
+                )
+                nc.tensor.matmul(
+                    out=s_ps[:, i * P : width], lhsT=ident_bf[:], rhs=mask_bf[:], start=False, stop=True
+                )
+                unused = rows.tile([P, T], BF16)
+                nc.vector.tensor_scalar(
+                    out=unused[:, 0:width],
+                    in0=s_ps[:, 0:width],
+                    scalar1=-SCALE,
+                    scalar2=None,
+                    op0=ALU.mult,
+                    op1=ALU.min,
+                    accum_out=shift[:, i : i + 1],
+                )
+                e_blk = rows.tile([P, T], BF16)
+                nc.scalar.activation(
+                    out=e_blk[:, 0:width],
+                    in_=s_ps[:, 0:width],
+                    func=ACT.Exp,
+                    bias=shift[:, i : i + 1],
+                    scale=SCALE,
+                    accum_out=rowsum[:, i : i + 1],
+                )
+                e_rows.append(e_blk)
+            rinv = small.tile([P, BLOCKS], F32)
+            nc.vector.reciprocal(out=rinv[:], in_=rowsum[:])
+            return e_rows, rinv
+
+        def quantise_e_and_v(index, head, e_rows, rinv):
+            b, h, n = head
+            r_ps = ps_misc.tile([P, T], F32, tag="r")
+            for i in range(BLOCKS):
+                nc.tensor.transpose(
+                    r_ps[:, i * P : (i + 1) * P], rinv[:, i : i + 1].to_broadcast([P, P]), ident_f32[:]
+                )
+            r_sb = handoff.tile([P, T], F32)
+            nc.scalar.copy(out=r_sb[:], in_=r_ps[:])
+
+            e_grouped = grouped_e[index % len(grouped_e)]
+            for i in range(BLOCKS):
+                et_ps = ps_et.tile([P, BLOCKS, P], BF16)
+                for j in range(i + 1):
+                    nc.tensor.transpose(et_ps[:, j, :], e_rows[i][:, j * P : (j + 1) * P], ident_bf[:])
+                nc.scalar.copy(
+                    out=e_grouped[:, i * P : (i + 1) * P, 0 : i + 1],
+                    in_=et_ps[:, 0 : i + 1, :].rearrange("p j t -> p t j"),
+                )
+            e_codes = handoff.tile([P, T], U32, align_bytes=64)
+            e_scales = handoff.tile([P, T], U8, align_bytes=64)
+            nc.vector.quantize_mx(
+                out=e_codes[:].bitcast(FP8X4),
+                scales=e_scales[:],
+                in_=e_grouped[:].rearrange("p t j -> p (t j)"),
+            )
+
+            v_ps = ps_misc.tile([P, PACK, DH], F32, tag="v")
+            for j in range(PACK):
+                steps = slice(n * T + j * P, n * T + (j + 1) * P)
+                for g in range(PASSES):
+                    nc.tensor.matmul_mx(
+                        out=v_ps[:, j, :],
+                        lhsT=x_codes[:, b, g, steps].bitcast(FP8X4),
+                        lhsT_scale=x_scales[:, b, g, steps],
+                        rhs=w_codes[:, h, g, :].bitcast(FP8X4),
+                        rhs_scale=w_scales[:, h, g, :],
+                        start=(g == 0),
+                        stop=(g == PASSES - 1),
+                    )
+            v_grouped = stage.tile([P, DH, PACK], BF16, align_bytes=64)
+            nc.vector.tensor_tensor(
+                out=v_grouped[:],
+                in0=v_ps[:].rearrange("p j c -> p c j"),
+                in1=bias_all[:, h * DH : (h + 1) * DH].unsqueeze(2).to_broadcast([P, DH, PACK]),
+                op=ALU.add,
+            )
+            v_codes = handoff.tile([P, DH], U32, align_bytes=64)
+            v_scales = handoff.tile([P, DH], U8, align_bytes=64)
+            nc.vector.quantize_mx(
+                out=v_codes[:].bitcast(FP8X4),
+                scales=v_scales[:],
+                in_=v_grouped[:].rearrange("p c j -> p (c j)"),
+            )
+            return r_sb, e_codes, e_scales, v_codes, v_scales
+
+        def attend(head, r_sb, e_codes, e_scales, v_codes, v_scales):
+            b, h, n = head
+            o_ps = ps_misc.tile([P, T], F32, tag="o")
+            nc.tensor.matmul_mx(
+                out=o_ps[:],
+                lhsT=v_codes[:].bitcast(FP8X4),
+                lhsT_scale=v_scales[:],
+                rhs=e_codes[:].bitcast(FP8X4),
+                rhs_scale=e_scales[:],
+                start=True,
+                stop=True,
+            )
+            o_sb = handoff.tile([P, T], F32)
+            nc.vector.tensor_tensor(out=o_sb[:], in0=o_ps[:], in1=r_sb[:], op=ALU.mult)
+            nc.gpsimd.dma_start(out=out[b, h * DH : (h + 1) * DH, n, :], in_=o_sb[:])
+
+        softmaxed = {}
+        operands = {}
+        for step in range(len(heads) + 2):
+            if step < len(heads):
+                softmaxed[step] = softmax_rows(heads[step])
+            if 0 <= step - 1 < len(heads):
+                b, h, n = heads[step - 1]
+                if h == 0:
+                    quantise_xin(b, n)
+                if b == 0 and n == 0:
+                    quantise_wv(h)
+                operands[step - 1] = quantise_e_and_v(step - 1, heads[step - 1], *softmaxed.pop(step - 1))
+            if 0 <= step - 2:
+                attend(heads[step - 2], *operands.pop(step - 2))

@@ -18,6 +18,8 @@ B, NODES, T, HEADS, DH = 2, 2, 512, 8, 128
 CIN = 1024
 PASSES = CIN // (P * PACK)
 BLOCKS = T // P
+PAIR = 2
+HALVES = PACK // PAIR
 SCALE = 1.0 / math.sqrt(DH)
 MASK_ADDEND = -(2.0**19)
 
@@ -31,7 +33,7 @@ def tile_tatt_pa_kernel(tc, x, tem_embedding, Wv, bv, q, k, out):
     with ExitStack() as ctx:
         keep = ctx.enter_context(tc.tile_pool(name="keep", bufs=1))
         stage = ctx.enter_context(tc.tile_pool(name="stage", bufs=2))
-        rows = ctx.enter_context(tc.tile_pool(name="rows", bufs=2 * BLOCKS))
+        rows = ctx.enter_context(tc.tile_pool(name="rows", bufs=BLOCKS))
         small = ctx.enter_context(tc.tile_pool(name="small", bufs=3))
         handoff = ctx.enter_context(tc.tile_pool(name="handoff", bufs=3))
         ps_scores = ctx.enter_context(tc.psum_pool(name="ps_scores", bufs=3))
@@ -84,11 +86,9 @@ def tile_tatt_pa_kernel(tc, x, tem_embedding, Wv, bv, q, k, out):
         mask_bf = keep.tile([P, P], BF16)
         nc.vector.tensor_copy(out=mask_bf[:], in_=mask_f32[:])
 
-        grouped_e = [
-            keep.tile([P, T, PACK], BF16, align_bytes=64, name="grouped_e%d" % r) for r in range(2)
-        ]
-        for tile_e in grouped_e:
-            nc.vector.memset(tile_e[:], 0.0)
+        e_buffers = [keep.tile([P, BLOCKS, T], BF16, name="e_rows%d" % r) for r in range(3)]
+        for e_buffer in e_buffers:
+            nc.vector.memset(e_buffer[:], 0.0)
 
         x_codes = keep.tile([P, B, PASSES, NODES * T], U32, align_bytes=64)
         x_scales = keep.tile([P, B, PASSES, NODES * T], U8, align_bytes=64)
@@ -100,8 +100,8 @@ def tile_tatt_pa_kernel(tc, x, tem_embedding, Wv, bv, q, k, out):
             for g in range(PASSES):
                 x_grouped = stage.tile([P, T, PACK], BF16, align_bytes=64)
                 nc.vector.tensor_copy(
-                    out=x_grouped[:].rearrange("p (c i) j -> p c j i", i=4),
-                    in_=xin_raw[:, b, g, :, steps].rearrange("p j (c i) -> p c j i", i=4),
+                    out=x_grouped[:].rearrange("p (w r m) j -> p w r m j", w=HALVES, r=PAIR),
+                    in_=xin_raw[:, b, g, :, steps].rearrange("p j (w m r) -> p w r m j", w=HALVES, r=PAIR),
                 )
                 nc.vector.quantize_mx(
                     out=x_codes[:, b, g, steps].bitcast(FP8X4),
@@ -131,13 +131,13 @@ def tile_tatt_pa_kernel(tc, x, tem_embedding, Wv, bv, q, k, out):
                 in_=w_grouped[:],
             )
 
-        def softmax_rows(head):
+        def softmax_rows(index, head):
             b, h, n = head
+            e_rows = e_buffers[index % len(e_buffers)]
             q_head = q_all[:, b * HEADS + h, n * T : (n + 1) * T]
             k_head = k_all[:, b * HEADS + h, n * T : (n + 1) * T]
             shift = small.tile([P, BLOCKS], F32)
             rowsum = small.tile([P, BLOCKS], F32)
-            e_rows = []
             for i in range(BLOCKS):
                 width = (i + 1) * P
                 s_ps = ps_scores.tile([P, T], F32)
@@ -161,21 +161,19 @@ def tile_tatt_pa_kernel(tc, x, tem_embedding, Wv, bv, q, k, out):
                     op1=ALU.min,
                     accum_out=shift[:, i : i + 1],
                 )
-                e_blk = rows.tile([P, T], BF16)
                 nc.scalar.activation(
-                    out=e_blk[:, 0:width],
+                    out=e_rows[:, i, 0:width],
                     in_=s_ps[:, 0:width],
                     func=ACT.Exp,
                     bias=shift[:, i : i + 1],
                     scale=SCALE,
                     accum_out=rowsum[:, i : i + 1],
                 )
-                e_rows.append(e_blk)
             rinv = small.tile([P, BLOCKS], F32)
             nc.vector.reciprocal(out=rinv[:], in_=rowsum[:])
             return e_rows, rinv
 
-        def quantise_e_and_v(index, head, e_rows, rinv):
+        def quantise_e_and_v(head, e_rows, rinv):
             b, h, n = head
             r_ps = ps_misc.tile([P, T], F32, tag="r")
             for i in range(BLOCKS):
@@ -185,21 +183,25 @@ def tile_tatt_pa_kernel(tc, x, tem_embedding, Wv, bv, q, k, out):
             r_sb = handoff.tile([P, T], F32)
             nc.scalar.copy(out=r_sb[:], in_=r_ps[:])
 
-            e_grouped = grouped_e[index % len(grouped_e)]
-            for i in range(BLOCKS):
-                et_ps = ps_et.tile([P, BLOCKS, P], BF16)
-                for j in range(i + 1):
-                    nc.tensor.transpose(et_ps[:, j, :], e_rows[i][:, j * P : (j + 1) * P], ident_bf[:])
+            e_grouped = stage.tile([P, T * PACK], BF16, align_bytes=64)
+            e_grouped_words = e_grouped[:].bitcast(F32).rearrange("p (i t w) -> p i t w", i=BLOCKS, w=HALVES)
+            blocks_per_bank = 2
+            for first in range(0, BLOCKS, blocks_per_bank):
+                et_ps = ps_et.tile([P, blocks_per_bank, HALVES, P], F32)
+                for i in range(first, first + blocks_per_bank):
+                    e_words = e_rows[:, i, :].bitcast(F32)
+                    for w in range(HALVES):
+                        nc.tensor.transpose(et_ps[:, i - first, w, :], e_words[:, w * P : (w + 1) * P], ident_f32[:])
                 nc.scalar.copy(
-                    out=e_grouped[:, i * P : (i + 1) * P, 0 : i + 1],
-                    in_=et_ps[:, 0 : i + 1, :].rearrange("p j t -> p t j"),
+                    out=e_grouped_words[:, first : first + blocks_per_bank],
+                    in_=et_ps[:].rearrange("p i w t -> p i t w"),
                 )
             e_codes = handoff.tile([P, T], U32, align_bytes=64)
             e_scales = handoff.tile([P, T], U8, align_bytes=64)
             nc.vector.quantize_mx(
                 out=e_codes[:].bitcast(FP8X4),
                 scales=e_scales[:],
-                in_=e_grouped[:].rearrange("p t j -> p (t j)"),
+                in_=e_grouped[:],
             )
 
             v_ps = ps_misc.tile([P, PACK, DH], F32, tag="v")
@@ -251,13 +253,13 @@ def tile_tatt_pa_kernel(tc, x, tem_embedding, Wv, bv, q, k, out):
         operands = {}
         for step in range(len(heads) + 2):
             if step < len(heads):
-                softmaxed[step] = softmax_rows(heads[step])
+                softmaxed[step] = softmax_rows(step, heads[step])
             if 0 <= step - 1 < len(heads):
                 b, h, n = heads[step - 1]
                 if h == 0:
                     quantise_xin(b, n)
                 if b == 0 and n == 0:
                     quantise_wv(h)
-                operands[step - 1] = quantise_e_and_v(step - 1, heads[step - 1], *softmaxed.pop(step - 1))
+                operands[step - 1] = quantise_e_and_v(heads[step - 1], *softmaxed.pop(step - 1))
             if 0 <= step - 2:
                 attend(heads[step - 2], *operands.pop(step - 2))

@@ -26,6 +26,10 @@ MASK_ADDEND = -(2.0**19)
 FLOPS = 2 * B * NODES * T * CIN * HEADS * DH + 2 * (2 * B * NODES * HEADS * T * T * DH)
 
 
+SCORE_BANKS = (("bank_1", (1,)), ("bank_2_0", (2, 0)), ("bank_3", (3,)))
+FIRST_STEP_OF_BATCH_1_XIN = 6
+
+
 def tile_tatt_pa_kernel(tc, x, tem_embedding, Wv, bv, q, k, out):
     nc = tc.nc
     heads = [(b, h, n) for b in range(B) for h in range(HEADS) for n in range(NODES)]
@@ -33,11 +37,10 @@ def tile_tatt_pa_kernel(tc, x, tem_embedding, Wv, bv, q, k, out):
     with ExitStack() as ctx:
         keep = ctx.enter_context(tc.tile_pool(name="keep", bufs=1))
         stage = ctx.enter_context(tc.tile_pool(name="stage", bufs=2))
-        rows = ctx.enter_context(tc.tile_pool(name="rows", bufs=BLOCKS))
         small = ctx.enter_context(tc.tile_pool(name="small", bufs=3))
         handoff = ctx.enter_context(tc.tile_pool(name="handoff", bufs=3))
-        ps_scores = ctx.enter_context(tc.psum_pool(name="ps_scores", bufs=3))
-        ps_et = ctx.enter_context(tc.psum_pool(name="ps_et", bufs=2))
+        ps_scores = ctx.enter_context(tc.psum_pool(name="ps_scores", bufs=1))
+        ps_et = ctx.enter_context(tc.psum_pool(name="ps_et", bufs=1))
         ps_misc = ctx.enter_context(tc.psum_pool(name="ps_misc", bufs=1))
 
         q_all = keep.tile([P, B * HEADS, NODES * T], BF16)
@@ -51,20 +54,26 @@ def tile_tatt_pa_kernel(tc, x, tem_embedding, Wv, bv, q, k, out):
             nc.sync.dma_start(out=q_all[:, b * HEADS + h, :], in_=q[b, channels].rearrange("c n t -> c (n t)"))
             nc.sync.dma_start(out=k_all[:, b * HEADS + h, :], in_=k[b, channels].rearrange("c n t -> c (n t)"))
 
-        def load_xin(b):
+        def load_wv(h):
+            nc.sync.dma_start(out=wv_raw[:, h, :], in_=Wv[h * DH : (h + 1) * DH, :])
+
+        def load_xin(b, n):
             for g, stream in enumerate((x, tem_embedding)):
                 nc.sync.dma_start(
-                    out=xin_raw[:, b, g], in_=stream[b].rearrange("(p j) n t -> p j (n t)", j=PACK)
+                    out=xin_raw[:, b, g, :, n * T : (n + 1) * T],
+                    in_=stream[b, :, n, :].rearrange("(p j) t -> p j t", j=PACK),
                 )
 
         nc.gpsimd.dma_start(out=bias_all[:], in_=bv.partition_broadcast(P))
         load_qk(0, 0)
-        load_xin(0)
-        for h in range(HEADS):
-            nc.sync.dma_start(out=wv_raw[:, h, :], in_=Wv[h * DH : (h + 1) * DH, :])
-            if h > 0:
-                load_qk(0, h)
-        load_xin(1)
+        load_wv(0)
+        load_xin(0, 0)
+        load_xin(0, 1)
+        for h in range(1, HEADS):
+            load_wv(h)
+            load_qk(0, h)
+        load_xin(1, 0)
+        load_xin(1, 1)
         for h in range(HEADS):
             load_qk(1, h)
 
@@ -86,7 +95,7 @@ def tile_tatt_pa_kernel(tc, x, tem_embedding, Wv, bv, q, k, out):
         mask_bf = keep.tile([P, P], BF16)
         nc.vector.tensor_copy(out=mask_bf[:], in_=mask_f32[:])
 
-        e_buffers = [keep.tile([P, BLOCKS, T], BF16, name="e_rows%d" % r) for r in range(3)]
+        e_buffers = [keep.tile([P, BLOCKS, T], BF16, name="e_rows%d" % r) for r in range(2)]
         for e_buffer in e_buffers:
             nc.vector.memset(e_buffer[:], 0.0)
 
@@ -95,115 +104,149 @@ def tile_tatt_pa_kernel(tc, x, tem_embedding, Wv, bv, q, k, out):
         w_codes = keep.tile([P, HEADS, PASSES, DH], U32, align_bytes=64)
         w_scales = keep.tile([P, HEADS, PASSES, DH], U8, align_bytes=64)
 
-        def quantise_xin(b, n):
-            steps = slice(n * T, (n + 1) * T)
-            for g in range(PASSES):
-                x_grouped = stage.tile([P, T, PACK], BF16, align_bytes=64)
-                nc.vector.tensor_copy(
-                    out=x_grouped[:].rearrange("p (w r m) j -> p w r m j", w=HALVES, r=PAIR),
-                    in_=xin_raw[:, b, g, :, steps].rearrange("p j (w m r) -> p w r m j", w=HALVES, r=PAIR),
-                )
-                nc.vector.quantize_mx(
-                    out=x_codes[:, b, g, steps].bitcast(FP8X4),
-                    scales=x_scales[:, b, g, steps],
-                    in_=x_grouped[:].rearrange("p t j -> p (t j)"),
-                )
+        tiles = {}
 
-        def quantise_wv(h):
+        def regroup_xin(b, n, g, on_gpsimd):
+            x_grouped = stage.tile([P, T, PACK], BF16, align_bytes=64)
+            tiles["x_grouped", (b, n, g)] = x_grouped
+            ordered = x_grouped[:].rearrange("p (w r m) j -> p w r m j", w=HALVES, r=PAIR)
+            given = xin_raw[:, b, g, :, n * T : (n + 1) * T].rearrange("p j (w m r) -> p w r m j", w=HALVES, r=PAIR)
+            if on_gpsimd:
+                for w in range(HALVES):
+                    nc.gpsimd.tensor_scalar(
+                        out=ordered[:, w], in0=given[:, w], scalar1=1.0, scalar2=0.0, op0=ALU.mult, op1=ALU.add
+                    )
+            else:
+                nc.vector.tensor_copy(out=ordered, in_=given)
+
+        def quantise_xin(b, n, g):
+            steps = slice(n * T, (n + 1) * T)
+            nc.vector.quantize_mx(
+                out=x_codes[:, b, g, steps].bitcast(FP8X4),
+                scales=x_scales[:, b, g, steps],
+                in_=tiles.pop(("x_grouped", (b, n, g)))[:].rearrange("p t j -> p (t j)"),
+            )
+
+        def transpose_wv(h):
             words = wv_raw[:, h, :].bitcast(F32)
-            words_per_pass = P * PACK // 2
-            wt_ps = ps_misc.tile([P, PASSES, 2, DH], F32, tag="r")
+            words_per_pass = P * HALVES
+            wt_ps = ps_misc.tile([P, PASSES, HALVES, DH], F32, tag="v")
             for g in range(PASSES):
-                for half in range(2):
+                for half in range(HALVES):
                     nc.tensor.transpose(
                         wt_ps[:, g, half, :],
-                        words[:, g * words_per_pass + half : (g + 1) * words_per_pass : 2],
+                        words[:, g * words_per_pass + half : (g + 1) * words_per_pass : HALVES],
                         ident_f32[:],
                     )
             w_grouped = stage.tile([P, PASSES * DH * PACK], BF16, align_bytes=64)
+            tiles["w_grouped", h] = w_grouped
             nc.scalar.copy(
-                out=w_grouped[:].bitcast(F32).rearrange("p (g o half) -> p g o half", g=PASSES, half=2),
+                out=w_grouped[:].bitcast(F32).rearrange("p (g o half) -> p g o half", g=PASSES, half=HALVES),
                 in_=wt_ps[:].rearrange("p g half o -> p g o half"),
             )
+
+        def quantise_wv(h):
             nc.vector.quantize_mx(
                 out=w_codes[:, h].rearrange("p g o -> p (g o)").bitcast(FP8X4),
                 scales=w_scales[:, h].rearrange("p g o -> p (g o)"),
-                in_=w_grouped[:],
+                in_=tiles.pop(("w_grouped", h))[:],
             )
 
-        def softmax_rows(index, head):
-            b, h, n = head
-            e_rows = e_buffers[index % len(e_buffers)]
+        def scores(s, bank_name, blocks):
+            b, h, n = heads[s]
             q_head = q_all[:, b * HEADS + h, n * T : (n + 1) * T]
             k_head = k_all[:, b * HEADS + h, n * T : (n + 1) * T]
-            shift = small.tile([P, BLOCKS], F32)
-            rowsum = small.tile([P, BLOCKS], F32)
-            for i in range(BLOCKS):
+            bank = ps_scores.tile([P, T], F32, tag=bank_name)
+            first_column = 0
+            for i in blocks:
                 width = (i + 1) * P
-                s_ps = ps_scores.tile([P, T], F32)
+                s_ps = bank[:, first_column : first_column + width]
+                first_column += width
                 nc.tensor.matmul(
-                    out=s_ps[:, 0:width],
-                    lhsT=q_head[:, i * P : (i + 1) * P],
-                    rhs=k_head[:, 0:width],
-                    start=True,
-                    stop=False,
+                    out=s_ps, lhsT=q_head[:, i * P : (i + 1) * P], rhs=k_head[:, 0:width], start=True, stop=False
                 )
                 nc.tensor.matmul(
                     out=s_ps[:, i * P : width], lhsT=ident_bf[:], rhs=mask_bf[:], start=False, stop=True
                 )
-                unused = rows.tile([P, T], BF16)
-                nc.vector.tensor_scalar(
-                    out=unused[:, 0:width],
-                    in0=s_ps[:, 0:width],
-                    scalar1=-SCALE,
-                    scalar2=None,
-                    op0=ALU.mult,
-                    op1=ALU.min,
-                    accum_out=shift[:, i : i + 1],
-                )
-                nc.scalar.activation(
-                    out=e_rows[:, i, 0:width],
-                    in_=s_ps[:, 0:width],
-                    func=ACT.Exp,
-                    bias=shift[:, i : i + 1],
-                    scale=SCALE,
-                    accum_out=rowsum[:, i : i + 1],
-                )
-            rinv = small.tile([P, BLOCKS], F32)
-            nc.vector.reciprocal(out=rinv[:], in_=rowsum[:])
-            return e_rows, rinv
+                tiles["s_ps", (s, i)] = s_ps
 
-        def quantise_e_and_v(head, e_rows, rinv):
-            b, h, n = head
+        def open_softmax(s):
+            tiles["shift", s] = small.tile([P, BLOCKS], F32, name="shift")
+            tiles["rowsum", s] = small.tile([P, BLOCKS], F32, name="rowsum")
+
+        def exp_block(s, i):
+            width = (i + 1) * P
+            s_ps = tiles.pop(("s_ps", (s, i)))
+            shift = tiles["shift", s][:, i : i + 1]
+            unused = handoff.tile([P, T], BF16)
+            nc.vector.tensor_scalar(
+                out=unused[:, 0:width],
+                in0=s_ps,
+                scalar1=-SCALE,
+                scalar2=None,
+                op0=ALU.mult,
+                op1=ALU.min,
+                accum_out=shift,
+            )
+            nc.scalar.activation(
+                out=e_buffers[s % len(e_buffers)][:, i, 0:width],
+                in_=s_ps,
+                func=ACT.Exp,
+                bias=shift,
+                scale=SCALE,
+                accum_out=tiles["rowsum", s][:, i : i + 1],
+            )
+
+        def spread_rinv(s):
+            rinv = small.tile([P, BLOCKS], F32)
+            nc.vector.reciprocal(out=rinv[:], in_=tiles.pop(("rowsum", s))[:])
             r_ps = ps_misc.tile([P, T], F32, tag="r")
             for i in range(BLOCKS):
                 nc.tensor.transpose(
                     r_ps[:, i * P : (i + 1) * P], rinv[:, i : i + 1].to_broadcast([P, P]), ident_f32[:]
                 )
-            r_sb = handoff.tile([P, T], F32)
-            nc.scalar.copy(out=r_sb[:], in_=r_ps[:])
+            tiles["r_ps", s] = r_ps
 
-            e_grouped = stage.tile([P, T * PACK], BF16, align_bytes=64)
-            e_grouped_words = e_grouped[:].bitcast(F32).rearrange("p (i t w) -> p i t w", i=BLOCKS, w=HALVES)
-            blocks_per_bank = 2
-            for first in range(0, BLOCKS, blocks_per_bank):
-                et_ps = ps_et.tile([P, blocks_per_bank, HALVES, P], F32)
-                for i in range(first, first + blocks_per_bank):
-                    e_words = e_rows[:, i, :].bitcast(F32)
-                    for w in range(HALVES):
-                        nc.tensor.transpose(et_ps[:, i - first, w, :], e_words[:, w * P : (w + 1) * P], ident_f32[:])
-                nc.scalar.copy(
-                    out=e_grouped_words[:, first : first + blocks_per_bank],
-                    in_=et_ps[:].rearrange("p i w t -> p i t w"),
-                )
+        def copy_rinv(s):
+            r_sb = handoff.tile([P, T], F32)
+            nc.scalar.copy(out=r_sb[:], in_=tiles.pop(("r_ps", s))[:])
+            tiles["r_sb", s] = r_sb
+
+        et_banks = {
+            0: ps_et.tile([P, 2, HALVES, P], F32, name="et_blocks_0_1"),
+            2: ps_et.tile([P, 2, HALVES, P], F32, name="et_blocks_2_3"),
+        }
+        zero_words = e_buffers[0][:, 0, T // 2 : T].bitcast(F32)
+        for i in range(2):
+            nc.tensor.transpose(et_banks[0][:, i, 1, :], zero_words, ident_f32[:])
+
+        def transpose_e(s, first):
+            for i in (first, first + 1):
+                e_words = e_buffers[s % len(e_buffers)][:, i, :].bitcast(F32)
+                for w in range(i // 2 + 1):
+                    nc.tensor.transpose(
+                        et_banks[first][:, i - first, w, :], e_words[:, w * P : (w + 1) * P], ident_f32[:]
+                    )
+
+        def copy_e(s, first):
+            if first == 0:
+                tiles["e_grouped", s] = stage.tile([P, T * PACK], BF16, align_bytes=64, name="e_grouped")
+            words = tiles["e_grouped", s][:].bitcast(F32).rearrange("p (i t w) -> p i t w", i=BLOCKS, w=HALVES)
+            nc.scalar.copy(
+                out=words[:, first : first + 2],
+                in_=et_banks[first][:].rearrange("p i w t -> p i t w"),
+            )
+
+        def quantise_e(s):
             e_codes = handoff.tile([P, T], U32, align_bytes=64)
             e_scales = handoff.tile([P, T], U8, align_bytes=64)
             nc.vector.quantize_mx(
-                out=e_codes[:].bitcast(FP8X4),
-                scales=e_scales[:],
-                in_=e_grouped[:],
+                out=e_codes[:].bitcast(FP8X4), scales=e_scales[:], in_=tiles.pop(("e_grouped", s))[:]
             )
+            tiles["e_mx", s] = (e_codes, e_scales)
 
+        def project_v(s):
+            b, h, n = heads[s]
             v_ps = ps_misc.tile([P, PACK, DH], F32, tag="v")
             for j in range(PACK):
                 steps = slice(n * T + j * P, n * T + (j + 1) * P)
@@ -217,24 +260,32 @@ def tile_tatt_pa_kernel(tc, x, tem_embedding, Wv, bv, q, k, out):
                         start=(g == 0),
                         stop=(g == PASSES - 1),
                     )
+            tiles["v_ps", s] = v_ps
+
+        def add_bias(s):
+            b, h, n = heads[s]
             v_grouped = stage.tile([P, DH, PACK], BF16, align_bytes=64)
             nc.vector.tensor_tensor(
                 out=v_grouped[:],
-                in0=v_ps[:].rearrange("p j c -> p c j"),
+                in0=tiles.pop(("v_ps", s))[:].rearrange("p j c -> p c j"),
                 in1=bias_all[:, h * DH : (h + 1) * DH].unsqueeze(2).to_broadcast([P, DH, PACK]),
                 op=ALU.add,
             )
+            tiles["v_grouped", s] = v_grouped
+
+        def quantise_v(s):
             v_codes = handoff.tile([P, DH], U32, align_bytes=64)
             v_scales = handoff.tile([P, DH], U8, align_bytes=64)
             nc.vector.quantize_mx(
                 out=v_codes[:].bitcast(FP8X4),
                 scales=v_scales[:],
-                in_=v_grouped[:].rearrange("p c j -> p (c j)"),
+                in_=tiles.pop(("v_grouped", s))[:].rearrange("p c j -> p (c j)"),
             )
-            return r_sb, e_codes, e_scales, v_codes, v_scales
+            tiles["v_mx", s] = (v_codes, v_scales)
 
-        def attend(head, r_sb, e_codes, e_scales, v_codes, v_scales):
-            b, h, n = head
+        def attend(s):
+            e_codes, e_scales = tiles.pop(("e_mx", s))
+            v_codes, v_scales = tiles.pop(("v_mx", s))
             o_ps = ps_misc.tile([P, T], F32, tag="o")
             nc.tensor.matmul_mx(
                 out=o_ps[:],
@@ -245,21 +296,72 @@ def tile_tatt_pa_kernel(tc, x, tem_embedding, Wv, bv, q, k, out):
                 start=True,
                 stop=True,
             )
+            tiles["o_ps", s] = o_ps
+
+        def normalise(s):
+            b, h, n = heads[s]
             o_sb = handoff.tile([P, T], F32)
-            nc.vector.tensor_tensor(out=o_sb[:], in0=o_ps[:], in1=r_sb[:], op=ALU.mult)
+            nc.vector.tensor_tensor(
+                out=o_sb[:], in0=tiles.pop(("o_ps", s))[:], in1=tiles.pop(("r_sb", s))[:], op=ALU.mult
+            )
             nc.gpsimd.dma_start(out=out[b, h * DH : (h + 1) * DH, n, :], in_=o_sb[:])
 
-        softmaxed = {}
-        operands = {}
-        for step in range(len(heads) + 2):
-            if step < len(heads):
-                softmaxed[step] = softmax_rows(step, heads[step])
-            if 0 <= step - 1 < len(heads):
-                b, h, n = heads[step - 1]
-                if h == 0:
-                    quantise_xin(b, n)
-                if b == 0 and n == 0:
-                    quantise_wv(h)
-                operands[step - 1] = quantise_e_and_v(heads[step - 1], *softmaxed.pop(step - 1))
-            if 0 <= step - 2:
-                attend(heads[step - 2], *operands.pop(step - 2))
+        def is_head(s):
+            return 0 <= s < len(heads)
+
+        def one_step(s):
+            if is_head(s - 1):
+                transpose_e(s - 1, 2)
+                project_v(s - 1)
+            if is_head(s - 2):
+                attend(s - 2)
+            if is_head(s - 1):
+                copy_e(s - 1, 0)
+            if is_head(s):
+                open_softmax(s)
+                exp_block(s, 0)
+                exp_block(s, 1)
+            if is_head(s + 1):
+                scores(s + 1, *SCORE_BANKS[0])
+            if is_head(s):
+                transpose_e(s, 0)
+            if is_head(s - 1):
+                copy_e(s - 1, 2)
+            if is_head(s):
+                exp_block(s, 2)
+            if is_head(s + 1):
+                scores(s + 1, *SCORE_BANKS[1])
+            if is_head(s):
+                exp_block(s, 3)
+            if is_head(s + 1):
+                scores(s + 1, *SCORE_BANKS[2])
+            if is_head(s - 1):
+                copy_rinv(s - 1)
+
+            if s % 2 == 0 and s // 2 < HEADS:
+                quantise_wv(s // 2)
+            if s in (0, 1):
+                for g in range(PASSES):
+                    regroup_xin(0, s, g, on_gpsimd=False)
+                for g in range(PASSES):
+                    quantise_xin(0, s, g)
+            unit = s - FIRST_STEP_OF_BATCH_1_XIN
+            if 0 <= unit - 1 < NODES * PASSES:
+                quantise_xin(1, *divmod(unit - 1, PASSES))
+            if 0 <= unit < NODES * PASSES:
+                regroup_xin(1, *divmod(unit, PASSES), on_gpsimd=True)
+
+            if is_head(s - 1):
+                add_bias(s - 1)
+                quantise_e(s - 1)
+                quantise_v(s - 1)
+            if s % 2 == 1 and (s + 1) // 2 < HEADS:
+                transpose_wv((s + 1) // 2)
+            if is_head(s):
+                spread_rinv(s)
+            if is_head(s - 2):
+                normalise(s - 2)
+
+        with tc.manual_schedule():
+            for s in range(-1, len(heads) + 2):
+                one_step(s)

@@ -26,7 +26,7 @@ MASK_ADDEND = -(2.0**19)
 FLOPS = 2 * B * NODES * T * CIN * HEADS * DH + 2 * (2 * B * NODES * HEADS * T * T * DH)
 
 
-SCORE_BANKS = (("bank_1", (1,)), ("bank_2_0", (2, 0)), ("bank_3", (3,)))
+SCORE_BANKS = (("bank_2_0", (2, 0)), ("bank_1", (1,)), ("bank_3", (3,)))
 FIRST_STEP_OF_BATCH_1_XIN = 6
 
 
@@ -171,35 +171,39 @@ def tile_tatt_pa_kernel(tc, x, tem_embedding, Wv, bv, q, k, out):
                 tiles["s_ps", (s, i)] = s_ps
 
         def open_softmax(s):
+            tiles["negated", s] = stage.tile([P, BLOCKS, T], F32, name="negated")
             tiles["shift", s] = small.tile([P, BLOCKS], F32, name="shift")
             tiles["rowsum", s] = small.tile([P, BLOCKS], F32, name="rowsum")
 
-        def exp_block(s, i):
-            width = (i + 1) * P
-            s_ps = tiles.pop(("s_ps", (s, i)))
-            shift = tiles["shift", s][:, i : i + 1]
-            unused = handoff.tile([P, T], BF16)
+        def rowmax(s, i):
             nc.vector.tensor_scalar(
-                out=unused[:, 0:width],
-                in0=s_ps,
+                out=tiles["negated", s][:, i, 0 : (i + 1) * P],
+                in0=tiles.pop(("s_ps", (s, i))),
                 scalar1=-SCALE,
                 scalar2=None,
                 op0=ALU.mult,
                 op1=ALU.min,
-                accum_out=shift,
+                accum_out=tiles["shift", s][:, i : i + 1],
             )
+
+        def exp_block(s, i):
+            width = (i + 1) * P
             nc.scalar.activation(
                 out=e_buffers[s % len(e_buffers)][:, i, 0:width],
-                in_=s_ps,
+                in_=tiles["negated", s][:, i, 0:width],
                 func=ACT.Exp,
-                bias=shift,
-                scale=SCALE,
+                bias=tiles["shift", s][:, i : i + 1],
+                scale=-1.0,
                 accum_out=tiles["rowsum", s][:, i : i + 1],
             )
 
-        def spread_rinv(s):
+        def reciprocal_rowsum(s):
             rinv = small.tile([P, BLOCKS], F32)
             nc.vector.reciprocal(out=rinv[:], in_=tiles.pop(("rowsum", s))[:])
+            tiles["rinv", s] = rinv
+
+        def spread_rinv(s):
+            rinv = tiles.pop(("rinv", s))
             r_ps = ps_misc.tile([P, T], F32, tag="r")
             for i in range(BLOCKS):
                 nc.tensor.transpose(
@@ -311,33 +315,30 @@ def tile_tatt_pa_kernel(tc, x, tem_embedding, Wv, bv, q, k, out):
 
         def one_step(s):
             if is_head(s - 1):
-                transpose_e(s - 1, 2)
                 project_v(s - 1)
-            if is_head(s - 2):
-                attend(s - 2)
-            if is_head(s - 1):
-                copy_e(s - 1, 0)
+            if is_head(s - 3):
+                attend(s - 3)
             if is_head(s):
                 open_softmax(s)
-                exp_block(s, 0)
-                exp_block(s, 1)
+                for i in (2, 0, 1, 3):
+                    rowmax(s, i)
+            if is_head(s - 1):
+                transpose_e(s - 1, 0)
+                transpose_e(s - 1, 2)
+            if is_head(s - 2):
+                spread_rinv(s - 2)
+            if is_head(s):
+                for i in (2, 0, 1, 3):
+                    exp_block(s, i)
+            if is_head(s - 1):
+                add_bias(s - 1)
             if is_head(s + 1):
                 scores(s + 1, *SCORE_BANKS[0])
-            if is_head(s):
-                transpose_e(s, 0)
-            if is_head(s - 1):
-                copy_e(s - 1, 2)
-            if is_head(s):
-                exp_block(s, 2)
+            if s % 2 == 1 and (s + 1) // 2 < HEADS:
+                transpose_wv((s + 1) // 2)
             if is_head(s + 1):
                 scores(s + 1, *SCORE_BANKS[1])
-            if is_head(s):
-                exp_block(s, 3)
-            if is_head(s + 1):
                 scores(s + 1, *SCORE_BANKS[2])
-            if is_head(s - 1):
-                copy_rinv(s - 1)
-
             if s % 2 == 0 and s // 2 < HEADS:
                 quantise_wv(s // 2)
             if s in (0, 1):
@@ -350,18 +351,19 @@ def tile_tatt_pa_kernel(tc, x, tem_embedding, Wv, bv, q, k, out):
                 quantise_xin(1, *divmod(unit - 1, PASSES))
             if 0 <= unit < NODES * PASSES:
                 regroup_xin(1, *divmod(unit, PASSES), on_gpsimd=True)
-
-            if is_head(s - 1):
-                add_bias(s - 1)
-                quantise_e(s - 1)
-                quantise_v(s - 1)
-            if s % 2 == 1 and (s + 1) // 2 < HEADS:
-                transpose_wv((s + 1) // 2)
-            if is_head(s):
-                spread_rinv(s)
             if is_head(s - 2):
-                normalise(s - 2)
+                quantise_e(s - 2)
+            if is_head(s - 1):
+                quantise_v(s - 1)
+                reciprocal_rowsum(s - 1)
+            if is_head(s - 3):
+                normalise(s - 3)
+            if is_head(s - 1):
+                copy_e(s - 1, 0)
+                copy_e(s - 1, 2)
+            if is_head(s - 2):
+                copy_rinv(s - 2)
 
         with tc.manual_schedule():
-            for s in range(-1, len(heads) + 2):
+            for s in range(-1, len(heads) + 3):
                 one_step(s)

@@ -28,6 +28,7 @@ FLOPS = 2 * B * NODES * T * CIN * HEADS * DH + 2 * (2 * B * NODES * HEADS * T * 
 
 SCORE_BANKS = (("bank_2_0", (2, 0)), ("bank_1", (1,)), ("bank_3", (3,)))
 FIRST_STEP_OF_BATCH_1_XIN = 6
+LOADED_AHEAD = 3
 
 
 def tile_tatt_pa_kernel(tc, x, tem_embedding, Wv, bv, q, k, out):
@@ -69,13 +70,18 @@ def tile_tatt_pa_kernel(tc, x, tem_embedding, Wv, bv, q, k, out):
         load_wv(0)
         load_xin(0, 0)
         load_xin(0, 1)
-        for h in range(1, HEADS):
+        for h in range(1, LOADED_AHEAD):
             load_wv(h)
             load_qk(0, h)
-        load_xin(1, 0)
-        load_xin(1, 1)
-        for h in range(HEADS):
-            load_qk(1, h)
+
+        def load_for_later(s):
+            if s % 2 == 0 and 0 <= s // 2 + LOADED_AHEAD < HEADS and s >= 0:
+                load_wv(s // 2 + LOADED_AHEAD)
+                load_qk(0, s // 2 + LOADED_AHEAD)
+            if s in (1, 3):
+                load_xin(1, s // 2)
+            if s % 2 == 1 and 0 <= (s - 5) // 2 < HEADS:
+                load_qk(1, (s - 5) // 2)
 
         ident_bf = keep.tile([P, P], BF16)
         make_identity(nc, ident_bf[:])
@@ -308,12 +314,13 @@ def tile_tatt_pa_kernel(tc, x, tem_embedding, Wv, bv, q, k, out):
             nc.vector.tensor_tensor(
                 out=o_sb[:], in0=tiles.pop(("o_ps", s))[:], in1=tiles.pop(("r_sb", s))[:], op=ALU.mult
             )
-            nc.gpsimd.dma_start(out=out[b, h * DH : (h + 1) * DH, n, :], in_=o_sb[:])
+            nc.sync.dma_start(out=out[b, h * DH : (h + 1) * DH, n, :], in_=o_sb[:])
 
         def is_head(s):
             return 0 <= s < len(heads)
 
         def one_step(s):
+            load_for_later(s)
             if is_head(s - 1):
                 project_v(s - 1)
             if is_head(s - 3):

@@ -26,8 +26,11 @@ MASK_ADDEND = -(2.0**19)
 FLOPS = 2 * B * NODES * T * CIN * HEADS * DH + 2 * (2 * B * NODES * HEADS * T * T * DH)
 
 
-SCORE_BANKS = (("bank_2_0", (2, 0)), ("bank_1", (1,)), ("bank_3", (3,)))
-FIRST_STEP_OF_BATCH_1_XIN = 6
+SCORE_BANKS = (("bank_3", (3,)), ("bank_2_0", (2, 0)), ("bank_1", (1,)))
+BLOCK_ORDER = (3, 2, 0, 1)
+PLACE = {3: 0, 2: 1, 0: 2, 1: 3}
+FIRST_STEP_OF_BATCH_1_XIN = 3
+QUARTERS = 4
 LOADED_AHEAD = 3
 
 
@@ -65,11 +68,18 @@ def tile_tatt_pa_kernel(tc, x, tem_embedding, Wv, bv, q, k, out):
                     in_=stream[b, :, n, :].rearrange("(p j) t -> p j t", j=PACK),
                 )
 
-        nc.gpsimd.dma_start(out=bias_all[:], in_=bv.partition_broadcast(P))
-        load_qk(0, 0)
-        load_wv(0)
+        def load_qk_node(b, h, n):
+            channels = slice(h * DH, (h + 1) * DH)
+            steps = slice(n * T, (n + 1) * T)
+            nc.sync.dma_start(out=q_all[:, b * HEADS + h, steps], in_=q[b, channels, n, :])
+            nc.sync.dma_start(out=k_all[:, b * HEADS + h, steps], in_=k[b, channels, n, :])
+
+        load_qk_node(0, 0, 0)
         load_xin(0, 0)
+        load_wv(0)
+        load_qk_node(0, 0, 1)
         load_xin(0, 1)
+        nc.sync.dma_start(out=bias_all[:], in_=bv.partition_broadcast(P))
         for h in range(1, LOADED_AHEAD):
             load_wv(h)
             load_qk(0, h)
@@ -112,18 +122,22 @@ def tile_tatt_pa_kernel(tc, x, tem_embedding, Wv, bv, q, k, out):
 
         tiles = {}
 
-        def regroup_xin(b, n, g, on_gpsimd):
-            x_grouped = stage.tile([P, T, PACK], BF16, align_bytes=64)
-            tiles["x_grouped", (b, n, g)] = x_grouped
-            ordered = x_grouped[:].rearrange("p (w r m) j -> p w r m j", w=HALVES, r=PAIR)
+        def grouped_view(b, n, g):
+            if ("x_grouped", (b, n, g)) not in tiles:
+                tiles["x_grouped", (b, n, g)] = stage.tile([P, T, PACK], BF16, align_bytes=64, name="x_grouped", bufs=3)
+            ordered = tiles["x_grouped", (b, n, g)][:].rearrange("p (w r m) j -> p w r m j", w=HALVES, r=PAIR)
             given = xin_raw[:, b, g, :, n * T : (n + 1) * T].rearrange("p j (w m r) -> p w r m j", w=HALVES, r=PAIR)
-            if on_gpsimd:
-                for w in range(HALVES):
-                    nc.gpsimd.tensor_scalar(
-                        out=ordered[:, w], in0=given[:, w], scalar1=1.0, scalar2=0.0, op0=ALU.mult, op1=ALU.add
-                    )
-            else:
-                nc.vector.tensor_copy(out=ordered, in_=given)
+            return ordered, given
+
+        def regroup_xin(b, n, g, copy):
+            ordered, given = grouped_view(b, n, g)
+            copy(out=ordered, in_=given)
+
+        def regroup_xin_piece(b, n, g, w, r):
+            ordered, given = grouped_view(b, n, g)
+            nc.gpsimd.tensor_scalar(
+                out=ordered[:, w, r], in0=given[:, w, r], scalar1=1.0, scalar2=0.0, op0=ALU.mult, op1=ALU.add
+            )
 
         def quantise_xin(b, n, g):
             steps = slice(n * T, (n + 1) * T)
@@ -136,7 +150,7 @@ def tile_tatt_pa_kernel(tc, x, tem_embedding, Wv, bv, q, k, out):
         def transpose_wv(h):
             words = wv_raw[:, h, :].bitcast(F32)
             words_per_pass = P * HALVES
-            wt_ps = ps_misc.tile([P, PASSES, HALVES, DH], F32, tag="v")
+            wt_ps = ps_misc.tile([P, PASSES, HALVES, DH], F32, tag="r")
             for g in range(PASSES):
                 for half in range(HALVES):
                     nc.tensor.transpose(
@@ -144,11 +158,14 @@ def tile_tatt_pa_kernel(tc, x, tem_embedding, Wv, bv, q, k, out):
                         words[:, g * words_per_pass + half : (g + 1) * words_per_pass : HALVES],
                         ident_f32[:],
                     )
+            tiles["wt_ps", h] = wt_ps
+
+        def copy_wv(h):
             w_grouped = stage.tile([P, PASSES * DH * PACK], BF16, align_bytes=64)
             tiles["w_grouped", h] = w_grouped
             nc.scalar.copy(
                 out=w_grouped[:].bitcast(F32).rearrange("p (g o half) -> p g o half", g=PASSES, half=HALVES),
-                in_=wt_ps[:].rearrange("p g half o -> p g o half"),
+                in_=tiles.pop(("wt_ps", h))[:].rearrange("p g half o -> p g o half"),
             )
 
         def quantise_wv(h):
@@ -177,30 +194,37 @@ def tile_tatt_pa_kernel(tc, x, tem_embedding, Wv, bv, q, k, out):
                 tiles["s_ps", (s, i)] = s_ps
 
         def open_softmax(s):
-            tiles["negated", s] = stage.tile([P, BLOCKS, T], F32, name="negated")
+            tiles["rowmax", s] = small.tile([P, BLOCKS], F32, name="row_maxima")
             tiles["shift", s] = small.tile([P, BLOCKS], F32, name="shift")
             tiles["rowsum", s] = small.tile([P, BLOCKS], F32, name="rowsum")
 
         def rowmax(s, i):
-            nc.vector.tensor_scalar(
-                out=tiles["negated", s][:, i, 0 : (i + 1) * P],
-                in0=tiles.pop(("s_ps", (s, i))),
+            nc.vector.tensor_reduce(
+                out=tiles["rowmax", s][:, PLACE[i] : PLACE[i] + 1],
+                in_=tiles["s_ps", (s, i)],
+                axis=mybir.AxisListType.X,
+                op=ALU.max,
+            )
+
+        def negate_maxima(s, blocks):
+            columns = slice(PLACE[blocks[0]], PLACE[blocks[-1]] + 1)
+            nc.gpsimd.tensor_scalar(
+                out=tiles["shift", s][:, columns],
+                in0=tiles["rowmax", s][:, columns],
                 scalar1=-SCALE,
-                scalar2=None,
+                scalar2=0.0,
                 op0=ALU.mult,
-                op1=ALU.min,
-                accum_out=tiles["shift", s][:, i : i + 1],
+                op1=ALU.add,
             )
 
         def exp_block(s, i):
-            width = (i + 1) * P
             nc.scalar.activation(
-                out=e_buffers[s % len(e_buffers)][:, i, 0:width],
-                in_=tiles["negated", s][:, i, 0:width],
+                out=e_buffers[s % len(e_buffers)][:, i, 0 : (i + 1) * P],
+                in_=tiles.pop(("s_ps", (s, i))),
                 func=ACT.Exp,
-                bias=tiles["shift", s][:, i : i + 1],
-                scale=-1.0,
-                accum_out=tiles["rowsum", s][:, i : i + 1],
+                bias=tiles["shift", s][:, PLACE[i] : PLACE[i] + 1],
+                scale=SCALE,
+                accum_out=tiles["rowsum", s][:, PLACE[i] : PLACE[i] + 1],
             )
 
         def reciprocal_rowsum(s):
@@ -213,7 +237,7 @@ def tile_tatt_pa_kernel(tc, x, tem_embedding, Wv, bv, q, k, out):
             r_ps = ps_misc.tile([P, T], F32, tag="r")
             for i in range(BLOCKS):
                 nc.tensor.transpose(
-                    r_ps[:, i * P : (i + 1) * P], rinv[:, i : i + 1].to_broadcast([P, P]), ident_f32[:]
+                    r_ps[:, i * P : (i + 1) * P], rinv[:, PLACE[i] : PLACE[i] + 1].to_broadcast([P, P]), ident_f32[:]
                 )
             tiles["r_ps", s] = r_ps
 
@@ -230,16 +254,16 @@ def tile_tatt_pa_kernel(tc, x, tem_embedding, Wv, bv, q, k, out):
         for i in range(2):
             nc.tensor.transpose(et_banks[0][:, i, 1, :], zero_words, ident_f32[:])
 
-        def transpose_e(s, first):
-            for i in (first, first + 1):
-                e_words = e_buffers[s % len(e_buffers)][:, i, :].bitcast(F32)
-                for w in range(i // 2 + 1):
-                    nc.tensor.transpose(
-                        et_banks[first][:, i - first, w, :], e_words[:, w * P : (w + 1) * P], ident_f32[:]
-                    )
+        def transpose_e(s, i):
+            first = i // 2 * 2
+            e_words = e_buffers[s % len(e_buffers)][:, i, :].bitcast(F32)
+            for w in range(i // 2 + 1):
+                nc.tensor.transpose(
+                    et_banks[first][:, i - first, w, :], e_words[:, w * P : (w + 1) * P], ident_f32[:]
+                )
 
         def copy_e(s, first):
-            if first == 0:
+            if first == 2:
                 tiles["e_grouped", s] = stage.tile([P, T * PACK], BF16, align_bytes=64, name="e_grouped")
             words = tiles["e_grouped", s][:].bitcast(F32).rearrange("p (i t w) -> p i t w", i=BLOCKS, w=HALVES)
             nc.scalar.copy(
@@ -321,56 +345,76 @@ def tile_tatt_pa_kernel(tc, x, tem_embedding, Wv, bv, q, k, out):
 
         def one_step(s):
             load_for_later(s)
-            if is_head(s - 1):
-                project_v(s - 1)
-            if is_head(s - 3):
-                attend(s - 3)
             if is_head(s):
                 open_softmax(s)
-                for i in (2, 0, 1, 3):
-                    rowmax(s, i)
-            if is_head(s - 1):
-                transpose_e(s - 1, 0)
-                transpose_e(s - 1, 2)
-            if is_head(s - 2):
-                spread_rinv(s - 2)
+                for bank_name, blocks in SCORE_BANKS:
+                    for i in blocks:
+                        rowmax(s, i)
+                    negate_maxima(s, blocks)
+            if s == 0:
+                copy_wv(0)
+                regroup_xin(0, 0, 0, nc.vector.tensor_copy)
+                regroup_xin(0, 0, 1, nc.scalar.copy)
+                regroup_xin(0, 1, 0, nc.vector.tensor_copy)
+                quantise_wv(0)
+                quantise_xin(0, 0, 0)
+                quantise_xin(0, 0, 1)
             if is_head(s):
-                for i in (2, 0, 1, 3):
+                for i in BLOCK_ORDER:
                     exp_block(s, i)
+            if s == 0:
+                regroup_xin(0, 1, 1, nc.scalar.copy)
+            if s == 1:
+                quantise_xin(0, 1, 0)
+                quantise_xin(0, 1, 1)
+            for piece in range(NODES * PASSES * QUARTERS):
+                if s == FIRST_STEP_OF_BATCH_1_XIN + piece * 3 // 4:
+                    unit, quarter = divmod(piece, QUARTERS)
+                    regroup_xin_piece(1, *divmod(unit, PASSES), *divmod(quarter, PAIR))
+            if is_head(s - 1):
+                reciprocal_rowsum(s - 1)
             if is_head(s - 1):
                 add_bias(s - 1)
+            if is_head(s):
+                transpose_e(s, 3)
             if is_head(s + 1):
                 scores(s + 1, *SCORE_BANKS[0])
-            if s % 2 == 1 and (s + 1) // 2 < HEADS:
-                transpose_wv((s + 1) // 2)
+            if is_head(s):
+                transpose_e(s, 2)
             if is_head(s + 1):
                 scores(s + 1, *SCORE_BANKS[1])
+            if is_head(s):
+                transpose_e(s, 0)
+                transpose_e(s, 1)
+            if is_head(s + 1):
                 scores(s + 1, *SCORE_BANKS[2])
-            if s % 2 == 0 and s // 2 < HEADS:
-                quantise_wv(s // 2)
-            if s in (0, 1):
-                for g in range(PASSES):
-                    regroup_xin(0, s, g, on_gpsimd=False)
-                for g in range(PASSES):
-                    quantise_xin(0, s, g)
-            unit = s - FIRST_STEP_OF_BATCH_1_XIN
-            if 0 <= unit - 1 < NODES * PASSES:
-                quantise_xin(1, *divmod(unit - 1, PASSES))
-            if 0 <= unit < NODES * PASSES:
-                regroup_xin(1, *divmod(unit, PASSES), on_gpsimd=True)
-            if is_head(s - 2):
-                quantise_e(s - 2)
+            if s % 2 == 1 and (s + 1) // 2 < HEADS and s > 0:
+                copy_wv((s + 1) // 2)
+            if is_head(s):
+                copy_e(s, 2)
+                copy_e(s, 0)
             if is_head(s - 1):
+                quantise_e(s - 1)
                 quantise_v(s - 1)
-                reciprocal_rowsum(s - 1)
-            if is_head(s - 3):
-                normalise(s - 3)
-            if is_head(s - 1):
-                copy_e(s - 1, 0)
-                copy_e(s - 1, 2)
             if is_head(s - 2):
-                copy_rinv(s - 2)
+                normalise(s - 2)
+            if s % 2 == 1 and (s + 1) // 2 < HEADS and s > 0:
+                quantise_wv((s + 1) // 2)
+            for unit in range(NODES * PASSES):
+                if s == FIRST_STEP_OF_BATCH_1_XIN + (unit + 1) * 3:
+                    quantise_xin(1, *divmod(unit, PASSES))
+            if is_head(s - 1):
+                spread_rinv(s - 1)
+                copy_rinv(s - 1)
+            if is_head(s):
+                project_v(s)
+            if is_head(s - 1):
+                attend(s - 1)
+            if s % 2 == 0 and s // 2 + 1 < HEADS and s >= 0:
+                transpose_wv(s // 2 + 1)
+            if s == -1:
+                transpose_wv(0)
 
         with tc.manual_schedule():
-            for s in range(-1, len(heads) + 3):
+            for s in range(-1, len(heads) + 2):
                 one_step(s)

@@ -28,7 +28,6 @@ FLOPS = 2 * B * NODES * T * CIN * HEADS * DH + 2 * (2 * B * NODES * HEADS * T * 
 
 SCORE_BANKS = (("bank_3", (3,)), ("bank_2_0", (2, 0)), ("bank_1", (1,)))
 BLOCK_ORDER = (3, 2, 0, 1)
-PLACE = {3: 0, 2: 1, 0: 2, 1: 3}
 FIRST_STEP_OF_BATCH_1_XIN = 3
 QUARTERS = 4
 LOADED_AHEAD = 3
@@ -194,37 +193,30 @@ def tile_tatt_pa_kernel(tc, x, tem_embedding, Wv, bv, q, k, out):
                 tiles["s_ps", (s, i)] = s_ps
 
         def open_softmax(s):
-            tiles["rowmax", s] = small.tile([P, BLOCKS], F32, name="row_maxima")
+            tiles["negated", s] = stage.tile([P, BLOCKS, T], F32, name="negated")
             tiles["shift", s] = small.tile([P, BLOCKS], F32, name="shift")
             tiles["rowsum", s] = small.tile([P, BLOCKS], F32, name="rowsum")
 
         def rowmax(s, i):
-            nc.vector.tensor_reduce(
-                out=tiles["rowmax", s][:, PLACE[i] : PLACE[i] + 1],
-                in_=tiles["s_ps", (s, i)],
-                axis=mybir.AxisListType.X,
-                op=ALU.max,
-            )
-
-        def negate_maxima(s, blocks):
-            columns = slice(PLACE[blocks[0]], PLACE[blocks[-1]] + 1)
-            nc.gpsimd.tensor_scalar(
-                out=tiles["shift", s][:, columns],
-                in0=tiles["rowmax", s][:, columns],
+            nc.vector.tensor_scalar(
+                out=tiles["negated", s][:, i, 0 : (i + 1) * P],
+                in0=tiles.pop(("s_ps", (s, i))),
                 scalar1=-SCALE,
-                scalar2=0.0,
+                scalar2=None,
                 op0=ALU.mult,
-                op1=ALU.add,
+                op1=ALU.min,
+                accum_out=tiles["shift", s][:, i : i + 1],
             )
 
         def exp_block(s, i):
+            width = (i + 1) * P
             nc.scalar.activation(
-                out=e_buffers[s % len(e_buffers)][:, i, 0 : (i + 1) * P],
-                in_=tiles.pop(("s_ps", (s, i))),
+                out=e_buffers[s % len(e_buffers)][:, i, 0:width],
+                in_=tiles["negated", s][:, i, 0:width],
                 func=ACT.Exp,
-                bias=tiles["shift", s][:, PLACE[i] : PLACE[i] + 1],
-                scale=SCALE,
-                accum_out=tiles["rowsum", s][:, PLACE[i] : PLACE[i] + 1],
+                bias=tiles["shift", s][:, i : i + 1],
+                scale=-1.0,
+                accum_out=tiles["rowsum", s][:, i : i + 1],
             )
 
         def reciprocal_rowsum(s):
@@ -237,7 +229,7 @@ def tile_tatt_pa_kernel(tc, x, tem_embedding, Wv, bv, q, k, out):
             r_ps = ps_misc.tile([P, T], F32, tag="r")
             for i in range(BLOCKS):
                 nc.tensor.transpose(
-                    r_ps[:, i * P : (i + 1) * P], rinv[:, PLACE[i] : PLACE[i] + 1].to_broadcast([P, P]), ident_f32[:]
+                    r_ps[:, i * P : (i + 1) * P], rinv[:, i : i + 1].to_broadcast([P, P]), ident_f32[:]
                 )
             tiles["r_ps", s] = r_ps
 
@@ -320,7 +312,10 @@ def tile_tatt_pa_kernel(tc, x, tem_embedding, Wv, bv, q, k, out):
         def attend(s):
             e_codes, e_scales = tiles.pop(("e_mx", s))
             v_codes, v_scales = tiles.pop(("v_mx", s))
-            o_ps = ps_misc.tile([P, T], F32, tag="o")
+            if s == len(heads) - 1:
+                o_ps = ps_scores.tile([P, T], F32, tag="bank_3")
+            else:
+                o_ps = ps_misc.tile([P, T], F32, tag="o")
             nc.tensor.matmul_mx(
                 out=o_ps[:],
                 lhsT=v_codes[:].bitcast(FP8X4),
@@ -347,32 +342,26 @@ def tile_tatt_pa_kernel(tc, x, tem_embedding, Wv, bv, q, k, out):
             load_for_later(s)
             if is_head(s):
                 open_softmax(s)
-                for bank_name, blocks in SCORE_BANKS:
-                    for i in blocks:
-                        rowmax(s, i)
-                    negate_maxima(s, blocks)
+                for i in BLOCK_ORDER:
+                    rowmax(s, i)
+            if is_head(s - 1):
+                reciprocal_rowsum(s - 1)
+            if s in (0, 1):
+                regroup_xin(0, s, 0, nc.vector.tensor_copy)
             if s == 0:
-                copy_wv(0)
-                regroup_xin(0, 0, 0, nc.vector.tensor_copy)
-                regroup_xin(0, 0, 1, nc.scalar.copy)
-                regroup_xin(0, 1, 0, nc.vector.tensor_copy)
-                quantise_wv(0)
+                regroup_xin(0, 0, 1, nc.vector.tensor_copy)
                 quantise_xin(0, 0, 0)
                 quantise_xin(0, 0, 1)
             if is_head(s):
                 for i in BLOCK_ORDER:
                     exp_block(s, i)
             if s == 0:
-                regroup_xin(0, 1, 1, nc.scalar.copy)
-            if s == 1:
-                quantise_xin(0, 1, 0)
-                quantise_xin(0, 1, 1)
+                copy_wv(0)
+                quantise_wv(0)
             for piece in range(NODES * PASSES * QUARTERS):
                 if s == FIRST_STEP_OF_BATCH_1_XIN + piece * 3 // 4:
                     unit, quarter = divmod(piece, QUARTERS)
                     regroup_xin_piece(1, *divmod(unit, PASSES), *divmod(quarter, PAIR))
-            if is_head(s - 1):
-                reciprocal_rowsum(s - 1)
             if is_head(s - 1):
                 add_bias(s - 1)
             if is_head(s):
@@ -386,34 +375,41 @@ def tile_tatt_pa_kernel(tc, x, tem_embedding, Wv, bv, q, k, out):
             if is_head(s):
                 transpose_e(s, 0)
                 transpose_e(s, 1)
+            if s == len(heads) - 1:
+                project_v(s)
             if is_head(s + 1):
                 scores(s + 1, *SCORE_BANKS[2])
-            if s % 2 == 1 and (s + 1) // 2 < HEADS and s > 0:
+            if s % 2 == 1 and 0 < (s + 1) // 2 < HEADS:
                 copy_wv((s + 1) // 2)
             if is_head(s):
                 copy_e(s, 2)
                 copy_e(s, 0)
+            if s == 0:
+                regroup_xin(0, 1, 1, nc.scalar.copy)
             if is_head(s - 1):
                 quantise_e(s - 1)
                 quantise_v(s - 1)
             if is_head(s - 2):
                 normalise(s - 2)
-            if s % 2 == 1 and (s + 1) // 2 < HEADS and s > 0:
-                quantise_wv((s + 1) // 2)
+            if s == 1:
+                quantise_xin(0, 1, 0)
+                quantise_xin(0, 1, 1)
+            if s % 2 == 0 and 0 < s // 2 < HEADS:
+                quantise_wv(s // 2)
             for unit in range(NODES * PASSES):
                 if s == FIRST_STEP_OF_BATCH_1_XIN + (unit + 1) * 3:
                     quantise_xin(1, *divmod(unit, PASSES))
             if is_head(s - 1):
                 spread_rinv(s - 1)
                 copy_rinv(s - 1)
-            if is_head(s):
+            if is_head(s) and s < len(heads) - 1:
                 project_v(s)
             if is_head(s - 1):
                 attend(s - 1)
-            if s % 2 == 0 and s // 2 + 1 < HEADS and s >= 0:
-                transpose_wv(s // 2 + 1)
             if s == -1:
                 transpose_wv(0)
+            if s % 2 == 0 and s >= 0 and s // 2 + 1 < HEADS:
+                transpose_wv(s // 2 + 1)
 
         with tc.manual_schedule():
             for s in range(-1, len(heads) + 2):

@@ -123,7 +123,7 @@ def tile_tatt_pa_kernel(tc, x, tem_embedding, Wv, bv, q, k, out):
 
         def grouped_view(b, n, g):
             if ("x_grouped", (b, n, g)) not in tiles:
-                tiles["x_grouped", (b, n, g)] = stage.tile([P, T, PACK], BF16, align_bytes=64, name="x_grouped", bufs=3)
+                tiles["x_grouped", (b, n, g)] = stage.tile([P, T, PACK], BF16, align_bytes=64, name="x_grouped", bufs=4)
             ordered = tiles["x_grouped", (b, n, g)][:].rearrange("p (w r m) j -> p w r m j", w=HALVES, r=PAIR)
             given = xin_raw[:, b, g, :, n * T : (n + 1) * T].rearrange("p j (w m r) -> p w r m j", w=HALVES, r=PAIR)
             return ordered, given
@@ -329,10 +329,53 @@ def tile_tatt_pa_kernel(tc, x, tem_embedding, Wv, bv, q, k, out):
 
         def normalise(s):
             b, h, n = heads[s]
-            o_sb = handoff.tile([P, T], F32)
+            o_sb = handoff.tile([P, T], F32, name="o_sb")
             nc.vector.tensor_tensor(
                 out=o_sb[:], in0=tiles.pop(("o_ps", s))[:], in1=tiles.pop(("r_sb", s))[:], op=ALU.mult
             )
+            nc.sync.dma_start(out=out[b, h * DH : (h + 1) * DH, n, :], in_=o_sb[:])
+
+        def turned(s):
+            return s % 5 == 1 and s < len(heads) - 2
+
+        def attend_turned(s):
+            e_codes, e_scales = tiles.pop(("e_mx", s))
+            v_codes, v_scales = tiles.pop(("v_mx", s))
+            o_ps = ps_misc.tile([P, BLOCKS, DH], F32, tag="o")
+            for i in range(BLOCKS):
+                rows = slice(i * P, (i + 1) * P)
+                nc.tensor.matmul_mx(
+                    out=o_ps[:, i, :],
+                    lhsT=e_codes[:, rows].bitcast(FP8X4),
+                    lhsT_scale=e_scales[:, rows],
+                    rhs=v_codes[:].bitcast(FP8X4),
+                    rhs_scale=v_scales[:],
+                    start=True,
+                    stop=True,
+                )
+            tiles["o_ps", s] = o_ps
+
+        def normalise_turned(s):
+            o_rows = handoff.tile([P, BLOCKS, DH], F32, name="o_rows")
+            rinv = tiles.pop(("rinv", s))
+            o_ps = tiles.pop(("o_ps", s))
+            for i in range(BLOCKS):
+                nc.scalar.activation(
+                    out=o_rows[:, i, :], in_=o_ps[:, i, :], func=ACT.Copy, scale=rinv[:, i : i + 1]
+                )
+            tiles["o_rows", s] = o_rows
+
+        def turn_back(s):
+            o_rows = tiles.pop(("o_rows", s))
+            o_ps = ps_misc.tile([P, T], F32, tag="o")
+            for i in range(BLOCKS):
+                nc.tensor.transpose(o_ps[:, i * P : (i + 1) * P], o_rows[:, i, :], ident_f32[:])
+            tiles["o_ps", s] = o_ps
+
+        def store_turned(s):
+            b, h, n = heads[s]
+            o_sb = handoff.tile([P, T], F32, name="o_sb")
+            nc.scalar.copy(out=o_sb[:], in_=tiles.pop(("o_ps", s))[:])
             nc.sync.dma_start(out=out[b, h * DH : (h + 1) * DH, n, :], in_=o_sb[:])
 
         def is_head(s):
@@ -346,66 +389,63 @@ def tile_tatt_pa_kernel(tc, x, tem_embedding, Wv, bv, q, k, out):
                     rowmax(s, i)
             if is_head(s - 1):
                 reciprocal_rowsum(s - 1)
-            if s in (0, 1):
-                regroup_xin(0, s, 0, nc.vector.tensor_copy)
             if s == 0:
-                regroup_xin(0, 0, 1, nc.vector.tensor_copy)
+                regroup_xin(0, 0, 0, nc.vector.tensor_copy)
+                regroup_xin(0, 0, 1, nc.scalar.copy)
+                copy_wv(0)
+                for g in range(PASSES):
+                    for quarter in range(QUARTERS):
+                        regroup_xin_piece(0, 1, g, *divmod(quarter, PAIR))
                 quantise_xin(0, 0, 0)
                 quantise_xin(0, 0, 1)
+                quantise_wv(0)
+            if s % 2 == 1 and 0 < (s + 1) // 2 < HEADS:
+                copy_wv((s + 1) // 2)
+            if is_head(s - 2) and turned(s - 2):
+                normalise_turned(s - 2)
             if is_head(s):
                 for i in BLOCK_ORDER:
                     exp_block(s, i)
-            if s == 0:
-                copy_wv(0)
-                quantise_wv(0)
             for piece in range(NODES * PASSES * QUARTERS):
                 if s == FIRST_STEP_OF_BATCH_1_XIN + piece * 3 // 4:
                     unit, quarter = divmod(piece, QUARTERS)
                     regroup_xin_piece(1, *divmod(unit, PASSES), *divmod(quarter, PAIR))
             if is_head(s - 1):
                 add_bias(s - 1)
-            if is_head(s):
-                transpose_e(s, 3)
+            if s % 2 == 0 and 0 < s // 2 < HEADS:
+                quantise_wv(s // 2)
             if is_head(s + 1):
-                scores(s + 1, *SCORE_BANKS[0])
+                for bank_name, blocks in SCORE_BANKS:
+                    scores(s + 1, bank_name, blocks)
+            if is_head(s - 1) and not turned(s - 1):
+                spread_rinv(s - 1)
+                copy_rinv(s - 1)
+            if is_head(s - 2) and turned(s - 2):
+                turn_back(s - 2)
+                store_turned(s - 2)
             if is_head(s):
-                transpose_e(s, 2)
-            if is_head(s + 1):
-                scores(s + 1, *SCORE_BANKS[1])
-            if is_head(s):
-                transpose_e(s, 0)
-                transpose_e(s, 1)
+                for i in BLOCK_ORDER:
+                    transpose_e(s, i)
             if s == len(heads) - 1:
                 project_v(s)
-            if is_head(s + 1):
-                scores(s + 1, *SCORE_BANKS[2])
-            if s % 2 == 1 and 0 < (s + 1) // 2 < HEADS:
-                copy_wv((s + 1) // 2)
             if is_head(s):
                 copy_e(s, 2)
                 copy_e(s, 0)
-            if s == 0:
-                regroup_xin(0, 1, 1, nc.scalar.copy)
             if is_head(s - 1):
                 quantise_e(s - 1)
                 quantise_v(s - 1)
-            if is_head(s - 2):
+            if is_head(s - 2) and not turned(s - 2):
                 normalise(s - 2)
             if s == 1:
                 quantise_xin(0, 1, 0)
                 quantise_xin(0, 1, 1)
-            if s % 2 == 0 and 0 < s // 2 < HEADS:
-                quantise_wv(s // 2)
             for unit in range(NODES * PASSES):
                 if s == FIRST_STEP_OF_BATCH_1_XIN + (unit + 1) * 3:
                     quantise_xin(1, *divmod(unit, PASSES))
-            if is_head(s - 1):
-                spread_rinv(s - 1)
-                copy_rinv(s - 1)
             if is_head(s) and s < len(heads) - 1:
                 project_v(s)
             if is_head(s - 1):
-                attend(s - 1)
+                (attend_turned if turned(s - 1) else attend)(s - 1)
             if s == -1:
                 transpose_wv(0)
             if s % 2 == 0 and s >= 0 and s // 2 + 1 < HEADS:

@@ -46,10 +46,12 @@ def tile_tatt_pa_kernel(tc, x, tem_embedding, Wv, bv, q, k, out):
         ps_et = ctx.enter_context(tc.psum_pool(name="ps_et", bufs=1))
         ps_misc = ctx.enter_context(tc.psum_pool(name="ps_misc", bufs=1))
 
+        ctx.enter_context(tc.manual_schedule())
+
         q_all = keep.tile([P, B * HEADS, NODES * T], BF16)
         k_all = keep.tile([P, B * HEADS, NODES * T], BF16)
         wv_raw = keep.tile([P, HEADS, CIN], BF16)
-        xin_raw = keep.tile([P, B, PASSES, PACK, NODES * T], BF16)
+        xin_raw = keep.tile([P, B, NODES, PASSES, PACK, T], BF16)
         bias_all = keep.tile([P, HEADS * DH], BF16)
 
         def load_qk(b, h):
@@ -58,12 +60,14 @@ def tile_tatt_pa_kernel(tc, x, tem_embedding, Wv, bv, q, k, out):
             nc.sync.dma_start(out=k_all[:, b * HEADS + h, :], in_=k[b, channels].rearrange("c n t -> c (n t)"))
 
         def load_wv(h):
-            nc.sync.dma_start(out=wv_raw[:, h, :], in_=Wv[h * DH : (h + 1) * DH, :])
+            channels = slice(h * DH, (h + 1) * DH)
+            nc.sync.dma_start(out=wv_raw[:, h, :], in_=Wv[channels, :])
+            nc.sync.dma_start(out=bias_all[:, channels], in_=bv[channels].partition_broadcast(P))
 
         def load_xin(b, n):
             for g, stream in enumerate((x, tem_embedding)):
                 nc.sync.dma_start(
-                    out=xin_raw[:, b, g, :, n * T : (n + 1) * T],
+                    out=xin_raw[:, b, n, g],
                     in_=stream[b, :, n, :].rearrange("(p j) t -> p j t", j=PACK),
                 )
 
@@ -78,7 +82,6 @@ def tile_tatt_pa_kernel(tc, x, tem_embedding, Wv, bv, q, k, out):
         load_wv(0)
         load_qk_node(0, 0, 1)
         load_xin(0, 1)
-        nc.sync.dma_start(out=bias_all[:], in_=bv.partition_broadcast(P))
         for h in range(1, LOADED_AHEAD):
             load_wv(h)
             load_qk(0, h)
@@ -92,10 +95,9 @@ def tile_tatt_pa_kernel(tc, x, tem_embedding, Wv, bv, q, k, out):
             if s % 2 == 1 and 0 <= (s - 5) // 2 < HEADS:
                 load_qk(1, (s - 5) // 2)
 
-        ident_bf = keep.tile([P, P], BF16)
-        make_identity(nc, ident_bf[:])
-        ident_f32 = keep.tile([P, P], F32)
-        make_identity(nc, ident_f32[:])
+        table_loader = keep.tile([P, 1], F32)
+        nc.vector.memset(table_loader[:], 0.0)
+        nc.scalar.activation(out=table_loader[:], in_=table_loader[:], func=ACT.Exp)
         mask_f32 = keep.tile([P, P], F32)
         nc.gpsimd.memset(mask_f32[:], 0.0)
         nc.gpsimd.affine_select(
@@ -109,10 +111,15 @@ def tile_tatt_pa_kernel(tc, x, tem_embedding, Wv, bv, q, k, out):
         )
         mask_bf = keep.tile([P, P], BF16)
         nc.vector.tensor_copy(out=mask_bf[:], in_=mask_f32[:])
+        ident_bf = keep.tile([P, P], BF16)
+        make_identity(nc, ident_bf[:])
+        ident_f32 = keep.tile([P, P], F32)
+        make_identity(nc, ident_f32[:])
 
         e_buffers = [keep.tile([P, BLOCKS, T], BF16, name="e_rows%d" % r) for r in range(2)]
         for e_buffer in e_buffers:
-            nc.vector.memset(e_buffer[:], 0.0)
+            nc.vector.memset(e_buffer[:, 0, P:T], 0.0)
+            nc.vector.memset(e_buffer[:, 2, 3 * P : T], 0.0)
 
         x_codes = keep.tile([P, B, PASSES, NODES * T], U32, align_bytes=64)
         x_scales = keep.tile([P, B, PASSES, NODES * T], U8, align_bytes=64)
@@ -125,7 +132,7 @@ def tile_tatt_pa_kernel(tc, x, tem_embedding, Wv, bv, q, k, out):
             if ("x_grouped", (b, n, g)) not in tiles:
                 tiles["x_grouped", (b, n, g)] = stage.tile([P, T, PACK], BF16, align_bytes=64, name="x_grouped", bufs=4)
             ordered = tiles["x_grouped", (b, n, g)][:].rearrange("p (w r m) j -> p w r m j", w=HALVES, r=PAIR)
-            given = xin_raw[:, b, g, :, n * T : (n + 1) * T].rearrange("p j (w m r) -> p w r m j", w=HALVES, r=PAIR)
+            given = xin_raw[:, b, n, g].rearrange("p j (w m r) -> p w r m j", w=HALVES, r=PAIR)
             return ordered, given
 
         def regroup_xin(b, n, g, copy):
@@ -242,9 +249,11 @@ def tile_tatt_pa_kernel(tc, x, tem_embedding, Wv, bv, q, k, out):
             0: ps_et.tile([P, 2, HALVES, P], F32, name="et_blocks_0_1"),
             2: ps_et.tile([P, 2, HALVES, P], F32, name="et_blocks_2_3"),
         }
-        zero_words = e_buffers[0][:, 0, T // 2 : T].bitcast(F32)
-        for i in range(2):
-            nc.tensor.transpose(et_banks[0][:, i, 1, :], zero_words, ident_f32[:])
+
+        def zero_masked_half():
+            zero_words = e_buffers[0][:, 0, T // 2 : T].bitcast(F32)
+            for i in range(2):
+                nc.tensor.transpose(et_banks[0][:, i, 1, :], zero_words, ident_f32[:])
 
         def transpose_e(s, i):
             first = i // 2 * 2
@@ -273,7 +282,10 @@ def tile_tatt_pa_kernel(tc, x, tem_embedding, Wv, bv, q, k, out):
 
         def project_v(s):
             b, h, n = heads[s]
-            v_ps = ps_misc.tile([P, PACK, DH], F32, tag="v")
+            if s == len(heads) - 1:
+                v_ps = ps_scores.tile([P, PACK, DH], F32, tag="bank_3")
+            else:
+                v_ps = ps_misc.tile([P, PACK, DH], F32, tag="v")
             for j in range(PACK):
                 steps = slice(n * T + j * P, n * T + (j + 1) * P)
                 for g in range(PASSES):
@@ -313,7 +325,7 @@ def tile_tatt_pa_kernel(tc, x, tem_embedding, Wv, bv, q, k, out):
             e_codes, e_scales = tiles.pop(("e_mx", s))
             v_codes, v_scales = tiles.pop(("v_mx", s))
             if s == len(heads) - 1:
-                o_ps = ps_scores.tile([P, T], F32, tag="bank_3")
+                o_ps = ps_scores.tile([P, T], F32, tag="bank_2_0")
             else:
                 o_ps = ps_misc.tile([P, T], F32, tag="o")
             nc.tensor.matmul_mx(
@@ -329,53 +341,10 @@ def tile_tatt_pa_kernel(tc, x, tem_embedding, Wv, bv, q, k, out):
 
         def normalise(s):
             b, h, n = heads[s]
-            o_sb = handoff.tile([P, T], F32, name="o_sb")
+            o_sb = handoff.tile([P, T], F32)
             nc.vector.tensor_tensor(
                 out=o_sb[:], in0=tiles.pop(("o_ps", s))[:], in1=tiles.pop(("r_sb", s))[:], op=ALU.mult
             )
-            nc.sync.dma_start(out=out[b, h * DH : (h + 1) * DH, n, :], in_=o_sb[:])
-
-        def turned(s):
-            return s % 5 == 1 and s < len(heads) - 2
-
-        def attend_turned(s):
-            e_codes, e_scales = tiles.pop(("e_mx", s))
-            v_codes, v_scales = tiles.pop(("v_mx", s))
-            o_ps = ps_misc.tile([P, BLOCKS, DH], F32, tag="o")
-            for i in range(BLOCKS):
-                rows = slice(i * P, (i + 1) * P)
-                nc.tensor.matmul_mx(
-                    out=o_ps[:, i, :],
-                    lhsT=e_codes[:, rows].bitcast(FP8X4),
-                    lhsT_scale=e_scales[:, rows],
-                    rhs=v_codes[:].bitcast(FP8X4),
-                    rhs_scale=v_scales[:],
-                    start=True,
-                    stop=True,
-                )
-            tiles["o_ps", s] = o_ps
-
-        def normalise_turned(s):
-            o_rows = handoff.tile([P, BLOCKS, DH], F32, name="o_rows")
-            rinv = tiles.pop(("rinv", s))
-            o_ps = tiles.pop(("o_ps", s))
-            for i in range(BLOCKS):
-                nc.scalar.activation(
-                    out=o_rows[:, i, :], in_=o_ps[:, i, :], func=ACT.Copy, scale=rinv[:, i : i + 1]
-                )
-            tiles["o_rows", s] = o_rows
-
-        def turn_back(s):
-            o_rows = tiles.pop(("o_rows", s))
-            o_ps = ps_misc.tile([P, T], F32, tag="o")
-            for i in range(BLOCKS):
-                nc.tensor.transpose(o_ps[:, i * P : (i + 1) * P], o_rows[:, i, :], ident_f32[:])
-            tiles["o_ps", s] = o_ps
-
-        def store_turned(s):
-            b, h, n = heads[s]
-            o_sb = handoff.tile([P, T], F32, name="o_sb")
-            nc.scalar.copy(out=o_sb[:], in_=tiles.pop(("o_ps", s))[:])
             nc.sync.dma_start(out=out[b, h * DH : (h + 1) * DH, n, :], in_=o_sb[:])
 
         def is_head(s):
@@ -401,8 +370,6 @@ def tile_tatt_pa_kernel(tc, x, tem_embedding, Wv, bv, q, k, out):
                 quantise_wv(0)
             if s % 2 == 1 and 0 < (s + 1) // 2 < HEADS:
                 copy_wv((s + 1) // 2)
-            if is_head(s - 2) and turned(s - 2):
-                normalise_turned(s - 2)
             if is_head(s):
                 for i in BLOCK_ORDER:
                     exp_block(s, i)
@@ -417,24 +384,21 @@ def tile_tatt_pa_kernel(tc, x, tem_embedding, Wv, bv, q, k, out):
             if is_head(s + 1):
                 for bank_name, blocks in SCORE_BANKS:
                     scores(s + 1, bank_name, blocks)
-            if is_head(s - 1) and not turned(s - 1):
+            if s == len(heads) - 1:
+                project_v(s)
+            if is_head(s - 1):
                 spread_rinv(s - 1)
                 copy_rinv(s - 1)
-            if is_head(s - 2) and turned(s - 2):
-                turn_back(s - 2)
-                store_turned(s - 2)
             if is_head(s):
                 for i in BLOCK_ORDER:
                     transpose_e(s, i)
-            if s == len(heads) - 1:
-                project_v(s)
             if is_head(s):
                 copy_e(s, 2)
                 copy_e(s, 0)
             if is_head(s - 1):
                 quantise_e(s - 1)
                 quantise_v(s - 1)
-            if is_head(s - 2) and not turned(s - 2):
+            if is_head(s - 2):
                 normalise(s - 2)
             if s == 1:
                 quantise_xin(0, 1, 0)
@@ -445,12 +409,12 @@ def tile_tatt_pa_kernel(tc, x, tem_embedding, Wv, bv, q, k, out):
             if is_head(s) and s < len(heads) - 1:
                 project_v(s)
             if is_head(s - 1):
-                (attend_turned if turned(s - 1) else attend)(s - 1)
+                attend(s - 1)
             if s == -1:
+                zero_masked_half()
                 transpose_wv(0)
             if s % 2 == 0 and s >= 0 and s // 2 + 1 < HEADS:
                 transpose_wv(s // 2 + 1)
 
-        with tc.manual_schedule():
-            for s in range(-1, len(heads) + 2):
-                one_step(s)
+        for s in range(-1, len(heads) + 2):
+            one_step(s)

@@ -28,8 +28,8 @@ FLOPS = 2 * B * NODES * T * CIN * HEADS * DH + 2 * (2 * B * NODES * HEADS * T * 
 
 SCORE_BANKS = (("bank_3", (3,)), ("bank_2_0", (2, 0)), ("bank_1", (1,)))
 BLOCK_ORDER = (3, 2, 0, 1)
-FIRST_STEP_OF_BATCH_1_XIN = 3
 QUARTERS = 4
+STEPS_OF_BATCH_1_XIN = [4, 5, 7, 8, 10, 11, 13, 14]
 LOADED_AHEAD = 3
 
 
@@ -62,7 +62,6 @@ def tile_tatt_pa_kernel(tc, x, tem_embedding, Wv, bv, q, k, out):
         def load_wv(h):
             channels = slice(h * DH, (h + 1) * DH)
             nc.sync.dma_start(out=wv_raw[:, h, :], in_=Wv[channels, :])
-            nc.sync.dma_start(out=bias_all[:, channels], in_=bv[channels].partition_broadcast(P))
 
         def load_xin(b, n):
             for g, stream in enumerate((x, tem_embedding)):
@@ -77,6 +76,9 @@ def tile_tatt_pa_kernel(tc, x, tem_embedding, Wv, bv, q, k, out):
             nc.sync.dma_start(out=q_all[:, b * HEADS + h, steps], in_=q[b, channels, n, :])
             nc.sync.dma_start(out=k_all[:, b * HEADS + h, steps], in_=k[b, channels, n, :])
 
+        bias_rows = keep.tile([P, HEADS * DH], BF16)
+        nc.vector.memset(bias_rows[:], 0.0)
+        nc.scalar.dma_start(out=bias_rows[0:1, :], in_=bv.unsqueeze(0))
         load_qk_node(0, 0, 0)
         load_xin(0, 0)
         load_wv(0)
@@ -111,6 +113,8 @@ def tile_tatt_pa_kernel(tc, x, tem_embedding, Wv, bv, q, k, out):
         )
         mask_bf = keep.tile([P, P], BF16)
         nc.vector.tensor_copy(out=mask_bf[:], in_=mask_f32[:])
+        ones_bf = keep.tile([P, P], BF16)
+        nc.vector.memset(ones_bf[:], 1.0)
         ident_bf = keep.tile([P, P], BF16)
         make_identity(nc, ident_bf[:])
         ident_f32 = keep.tile([P, P], F32)
@@ -139,10 +143,20 @@ def tile_tatt_pa_kernel(tc, x, tem_embedding, Wv, bv, q, k, out):
             ordered, given = grouped_view(b, n, g)
             copy(out=ordered, in_=given)
 
-        def regroup_xin_piece(b, n, g, w, r):
+        def give_way(s):
+            one = small.tile([P, 1], F32, name="one")
+            nc.vector.memset(one[:], 1.0)
+            tiles["one", s] = one
+
+        def regroup_xin_quarter(s, b, n, g, w, r):
             ordered, given = grouped_view(b, n, g)
             nc.gpsimd.tensor_scalar(
-                out=ordered[:, w, r], in0=given[:, w, r], scalar1=1.0, scalar2=0.0, op0=ALU.mult, op1=ALU.add
+                out=ordered[:, w, r],
+                in0=given[:, w, r],
+                scalar1=tiles["one", s][:],
+                scalar2=0.0,
+                op0=ALU.mult,
+                op1=ALU.add,
             )
 
         def quantise_xin(b, n, g):
@@ -250,6 +264,12 @@ def tile_tatt_pa_kernel(tc, x, tem_embedding, Wv, bv, q, k, out):
             2: ps_et.tile([P, 2, HALVES, P], F32, name="et_blocks_2_3"),
         }
 
+        def spread_bias(half):
+            columns = slice(half * T, (half + 1) * T)
+            bias_ps = ps_misc.tile([P, T], F32, tag="r")
+            nc.tensor.matmul(out=bias_ps[:], lhsT=ones_bf[:], rhs=bias_rows[:, columns], start=True, stop=True)
+            nc.scalar.copy(out=bias_all[:, columns], in_=bias_ps[:])
+
         def zero_masked_half():
             zero_words = e_buffers[0][:, 0, T // 2 : T].bitcast(F32)
             for i in range(2):
@@ -341,10 +361,28 @@ def tile_tatt_pa_kernel(tc, x, tem_embedding, Wv, bv, q, k, out):
 
         def normalise(s):
             b, h, n = heads[s]
-            o_sb = handoff.tile([P, T], F32)
+            o_sb = handoff.tile([P, T], F32, name="o_sb")
             nc.vector.tensor_tensor(
                 out=o_sb[:], in0=tiles.pop(("o_ps", s))[:], in1=tiles.pop(("r_sb", s))[:], op=ALU.mult
             )
+            nc.sync.dma_start(out=out[b, h * DH : (h + 1) * DH, n, :], in_=o_sb[:])
+
+        def on_gpsimd(s):
+            return s % 3 == 1 and s < len(heads) - 2
+
+        def bring_product(s):
+            o_raw = handoff.tile([P, T], F32, name="o_raw", bufs=2)
+            nc.scalar.copy(out=o_raw[:], in_=tiles.pop(("o_ps", s))[:])
+            tiles["o_raw", s] = o_raw
+
+        def normalise_on_gpsimd(s):
+            b, h, n = heads[s]
+            o_sb = handoff.tile([P, T], F32, name="o_sb")
+            o_raw = tiles.pop(("o_raw", s))
+            r_sb = tiles.pop(("r_sb", s))
+            for i in range(BLOCKS):
+                piece = slice(i * P, (i + 1) * P)
+                nc.gpsimd.tensor_tensor(out=o_sb[:, piece], in0=o_raw[:, piece], in1=r_sb[:, piece], op=ALU.mult)
             nc.sync.dma_start(out=out[b, h * DH : (h + 1) * DH, n, :], in_=o_sb[:])
 
         def is_head(s):
@@ -362,9 +400,7 @@ def tile_tatt_pa_kernel(tc, x, tem_embedding, Wv, bv, q, k, out):
                 regroup_xin(0, 0, 0, nc.vector.tensor_copy)
                 regroup_xin(0, 0, 1, nc.scalar.copy)
                 copy_wv(0)
-                for g in range(PASSES):
-                    for quarter in range(QUARTERS):
-                        regroup_xin_piece(0, 1, g, *divmod(quarter, PAIR))
+                regroup_xin(0, 1, 0, nc.vector.tensor_copy)
                 quantise_xin(0, 0, 0)
                 quantise_xin(0, 0, 1)
                 quantise_wv(0)
@@ -373,10 +409,9 @@ def tile_tatt_pa_kernel(tc, x, tem_embedding, Wv, bv, q, k, out):
             if is_head(s):
                 for i in BLOCK_ORDER:
                     exp_block(s, i)
-            for piece in range(NODES * PASSES * QUARTERS):
-                if s == FIRST_STEP_OF_BATCH_1_XIN + piece * 3 // 4:
-                    unit, quarter = divmod(piece, QUARTERS)
-                    regroup_xin_piece(1, *divmod(unit, PASSES), *divmod(quarter, PAIR))
+            if is_head(s - 2) and on_gpsimd(s - 2):
+                bring_product(s - 2)
+                normalise_on_gpsimd(s - 2)
             if is_head(s - 1):
                 add_bias(s - 1)
             if s % 2 == 0 and 0 < s // 2 < HEADS:
@@ -395,16 +430,25 @@ def tile_tatt_pa_kernel(tc, x, tem_embedding, Wv, bv, q, k, out):
             if is_head(s):
                 copy_e(s, 2)
                 copy_e(s, 0)
+            if s == 0:
+                regroup_xin(0, 1, 1, nc.scalar.copy)
+            if s == 2:
+                spread_bias(1)
             if is_head(s - 1):
                 quantise_e(s - 1)
                 quantise_v(s - 1)
-            if is_head(s - 2):
+            if s in STEPS_OF_BATCH_1_XIN:
+                give_way(s)
+                unit, half = divmod(STEPS_OF_BATCH_1_XIN.index(s), 2)
+                for quarter in range(half * 2, half * 2 + 2):
+                    regroup_xin_quarter(s, 1, *divmod(unit, PASSES), *divmod(quarter, PAIR))
+            if is_head(s - 2) and not on_gpsimd(s - 2):
                 normalise(s - 2)
             if s == 1:
                 quantise_xin(0, 1, 0)
                 quantise_xin(0, 1, 1)
             for unit in range(NODES * PASSES):
-                if s == FIRST_STEP_OF_BATCH_1_XIN + (unit + 1) * 3:
+                if s == STEPS_OF_BATCH_1_XIN[unit * 2 + 1] + 1:
                     quantise_xin(1, *divmod(unit, PASSES))
             if is_head(s) and s < len(heads) - 1:
                 project_v(s)
@@ -412,6 +456,7 @@ def tile_tatt_pa_kernel(tc, x, tem_embedding, Wv, bv, q, k, out):
                 attend(s - 1)
             if s == -1:
                 zero_masked_half()
+                spread_bias(0)
                 transpose_wv(0)
             if s % 2 == 0 and s >= 0 and s // 2 + 1 < HEADS:
                 transpose_wv(s // 2 + 1)

@@ -78,8 +78,8 @@ def tile_tatt_pa_kernel(tc, x, tem_embedding, Wv, bv, q, k, out):
 
         bias_rows = keep.tile([P, HEADS * DH], BF16)
         nc.vector.memset(bias_rows[:], 0.0)
-        nc.scalar.dma_start(out=bias_rows[0:1, :], in_=bv.unsqueeze(0))
         load_qk_node(0, 0, 0)
+        nc.sync.dma_start(out=bias_rows[0:1, :], in_=bv.unsqueeze(0))
         load_xin(0, 0)
         load_wv(0)
         load_qk_node(0, 0, 1)
@@ -390,6 +390,10 @@ def tile_tatt_pa_kernel(tc, x, tem_embedding, Wv, bv, q, k, out):
 
         def one_step(s):
             load_for_later(s)
+            if s == 1:
+                give_way(s)
+                for quarter in range(QUARTERS):
+                    regroup_xin_quarter(s, 0, 1, 1, *divmod(quarter, PAIR))
             if is_head(s):
                 open_softmax(s)
                 for i in BLOCK_ORDER:
@@ -430,8 +434,6 @@ def tile_tatt_pa_kernel(tc, x, tem_embedding, Wv, bv, q, k, out):
             if is_head(s):
                 copy_e(s, 2)
                 copy_e(s, 0)
-            if s == 0:
-                regroup_xin(0, 1, 1, nc.scalar.copy)
             if s == 2:
                 spread_bias(1)
             if is_head(s - 1):

@@ -18,6 +18,7 @@ B, NODES, T, HEADS, DH = 2, 2, 512, 8, 128
 CIN = 1024
 PASSES = CIN // (P * PACK)
 BLOCKS = T // P
+COPIES = P // BLOCKS
 PAIR = 2
 HALVES = PACK // PAIR
 SCALE = 1.0 / math.sqrt(DH)
@@ -29,7 +30,8 @@ FLOPS = 2 * B * NODES * T * CIN * HEADS * DH + 2 * (2 * B * NODES * HEADS * T * 
 SCORE_BANKS = (("bank_3", (3,)), ("bank_2_0", (2, 0)), ("bank_1", (1,)))
 BLOCK_ORDER = (3, 2, 0, 1)
 QUARTERS = 4
-STEPS_OF_BATCH_1_XIN = [4, 5, 7, 8, 10, 11, 13, 14]
+SHORT_WAY = 2
+STEPS_OF_BATCH_1_XIN = [3, 4, 6, 7, 9, 10, 12, 13]
 LOADED_AHEAD = 3
 
 
@@ -167,10 +169,10 @@ def tile_tatt_pa_kernel(tc, x, tem_embedding, Wv, bv, q, k, out):
                 in_=tiles.pop(("x_grouped", (b, n, g)))[:].rearrange("p t j -> p (t j)"),
             )
 
-        def transpose_wv(h):
+        def transpose_wv(h, pool, bank_name):
             words = wv_raw[:, h, :].bitcast(F32)
             words_per_pass = P * HALVES
-            wt_ps = ps_misc.tile([P, PASSES, HALVES, DH], F32, tag="r")
+            wt_ps = pool.tile([P, PASSES, HALVES, DH], F32, tag=bank_name)
             for g in range(PASSES):
                 for half in range(HALVES):
                     nc.tensor.transpose(
@@ -241,21 +243,55 @@ def tile_tatt_pa_kernel(tc, x, tem_embedding, Wv, bv, q, k, out):
             )
 
         def reciprocal_rowsum(s):
-            rinv = small.tile([P, BLOCKS], F32)
+            rinv = small.tile([P, BLOCKS], F32, name="rinv")
             nc.vector.reciprocal(out=rinv[:], in_=tiles.pop(("rowsum", s))[:])
             tiles["rinv", s] = rinv
+
+        def copies_in_hbm(s):
+            b, h, n = heads[s // 2 * 2 + 2]
+            first = h * DH + s % 2 * (DH // 2)
+            return out[b, first : first + DH // 2].rearrange("c n t -> (c n t)")
+
+        def repeat_rinv(s):
+            rinv_copies = small.tile([P, COPIES, BLOCKS], F32, name="rinv_copies")
+            nc.gpsimd.tensor_scalar(
+                out=rinv_copies[:],
+                in0=tiles.pop(("rinv", s))[:].unsqueeze(1).to_broadcast([P, COPIES, BLOCKS]),
+                scalar1=1.0,
+                scalar2=0.0,
+                op0=ALU.mult,
+                op1=ALU.add,
+            )
+            tiles["rinv_copies", s] = rinv_copies
+
+        def transpose_rinv(s):
+            r_ps = ps_misc.tile([P, T], F32, tag="r")
+            copies = tiles.pop(("rinv_copies", s))
+            nc.tensor.transpose(r_ps[:, 0:P], copies[:].rearrange("p k i -> p (k i)"), ident_f32[:])
+            tiles["r_ps", s] = r_ps
+
+        def park_rinv(s):
+            r_rows = handoff.tile([P, P], F32, name="r_rows")
+            nc.scalar.copy(out=r_rows[:], in_=tiles.pop(("r_ps", s))[:, 0:P])
+            nc.sync.dma_start(
+                out=copies_in_hbm(s).rearrange("(c p t) -> p c t", c=BLOCKS, p=P),
+                in_=r_rows[:].unsqueeze(1).to_broadcast([P, BLOCKS, P]),
+            )
+
+        def fetch_rinv(s):
+            r_sb = handoff.tile([P, T], F32, name="r_sb", bufs=4)
+            nc.sync.dma_start(out=r_sb[:], in_=copies_in_hbm(s).rearrange("(p t) -> p t", p=P))
+            tiles["r_sb", s] = r_sb
 
         def spread_rinv(s):
             rinv = tiles.pop(("rinv", s))
             r_ps = ps_misc.tile([P, T], F32, tag="r")
             for i in range(BLOCKS):
-                nc.tensor.transpose(
-                    r_ps[:, i * P : (i + 1) * P], rinv[:, i : i + 1].to_broadcast([P, P]), ident_f32[:]
-                )
+                nc.tensor.transpose(r_ps[:, i * P : (i + 1) * P], rinv[:, i : i + 1].to_broadcast([P, P]), ident_f32[:])
             tiles["r_ps", s] = r_ps
 
         def copy_rinv(s):
-            r_sb = handoff.tile([P, T], F32)
+            r_sb = handoff.tile([P, T], F32, name="r_sb", bufs=4)
             nc.scalar.copy(out=r_sb[:], in_=tiles.pop(("r_ps", s))[:])
             tiles["r_sb", s] = r_sb
 
@@ -344,8 +380,9 @@ def tile_tatt_pa_kernel(tc, x, tem_embedding, Wv, bv, q, k, out):
         def attend(s):
             e_codes, e_scales = tiles.pop(("e_mx", s))
             v_codes, v_scales = tiles.pop(("v_mx", s))
-            if s == len(heads) - 1:
-                o_ps = ps_scores.tile([P, T], F32, tag="bank_2_0")
+            o_bank = {len(heads) - 2: "bank_2_0", len(heads) - 1: "bank_1"}.get(s)
+            if o_bank:
+                o_ps = ps_scores.tile([P, T], F32, tag=o_bank)
             else:
                 o_ps = ps_misc.tile([P, T], F32, tag="o")
             nc.tensor.matmul_mx(
@@ -361,14 +398,14 @@ def tile_tatt_pa_kernel(tc, x, tem_embedding, Wv, bv, q, k, out):
 
         def normalise(s):
             b, h, n = heads[s]
-            o_sb = handoff.tile([P, T], F32, name="o_sb")
+            o_sb = handoff.tile([P, T], F32, name="o_sb", bufs=4)
             nc.vector.tensor_tensor(
                 out=o_sb[:], in0=tiles.pop(("o_ps", s))[:], in1=tiles.pop(("r_sb", s))[:], op=ALU.mult
             )
             nc.sync.dma_start(out=out[b, h * DH : (h + 1) * DH, n, :], in_=o_sb[:])
 
         def on_gpsimd(s):
-            return s % 3 == 1 and s < len(heads) - 2
+            return (s % 3 == 1 or (s % 3 == 2 and s >= 11)) and s < 27
 
         def bring_product(s):
             o_raw = handoff.tile([P, T], F32, name="o_raw", bufs=2)
@@ -377,7 +414,7 @@ def tile_tatt_pa_kernel(tc, x, tem_embedding, Wv, bv, q, k, out):
 
         def normalise_on_gpsimd(s):
             b, h, n = heads[s]
-            o_sb = handoff.tile([P, T], F32, name="o_sb")
+            o_sb = handoff.tile([P, T], F32, name="o_sb", bufs=4)
             o_raw = tiles.pop(("o_raw", s))
             r_sb = tiles.pop(("r_sb", s))
             for i in range(BLOCKS):
@@ -385,10 +422,20 @@ def tile_tatt_pa_kernel(tc, x, tem_embedding, Wv, bv, q, k, out):
                 nc.gpsimd.tensor_tensor(out=o_sb[:, piece], in0=o_raw[:, piece], in1=r_sb[:, piece], op=ALU.mult)
             nc.sync.dma_start(out=out[b, h * DH : (h + 1) * DH, n, :], in_=o_sb[:])
 
+        def takes_short_way(s):
+            return s >= len(heads) - SHORT_WAY
+
+        def multiplied_in(s):
+            long_way = [s - 3] if 0 <= s - 3 < len(heads) - SHORT_WAY else []
+            short_way = [s - 1] if is_head(s - 1) and takes_short_way(s - 1) else []
+            return short_way + long_way
+
         def is_head(s):
             return 0 <= s < len(heads)
 
         def one_step(s):
+            if 0 <= s - 3 and not takes_short_way(s - 3):
+                fetch_rinv(s - 3)
             load_for_later(s)
             if s == 1:
                 give_way(s)
@@ -400,6 +447,8 @@ def tile_tatt_pa_kernel(tc, x, tem_embedding, Wv, bv, q, k, out):
                     rowmax(s, i)
             if is_head(s - 1):
                 reciprocal_rowsum(s - 1)
+                if not takes_short_way(s - 1):
+                    repeat_rinv(s - 1)
             if s == 0:
                 regroup_xin(0, 0, 0, nc.vector.tensor_copy)
                 regroup_xin(0, 0, 1, nc.scalar.copy)
@@ -408,32 +457,44 @@ def tile_tatt_pa_kernel(tc, x, tem_embedding, Wv, bv, q, k, out):
                 quantise_xin(0, 0, 0)
                 quantise_xin(0, 0, 1)
                 quantise_wv(0)
-            if s % 2 == 1 and 0 < (s + 1) // 2 < HEADS:
-                copy_wv((s + 1) // 2)
             if is_head(s):
                 for i in BLOCK_ORDER:
                     exp_block(s, i)
-            if is_head(s - 2) and on_gpsimd(s - 2):
-                bring_product(s - 2)
-                normalise_on_gpsimd(s - 2)
+            for r in multiplied_in(s - 1):
+                if on_gpsimd(r):
+                    bring_product(r)
+                    normalise_on_gpsimd(r)
             if is_head(s - 1):
                 add_bias(s - 1)
             if s % 2 == 0 and 0 < s // 2 < HEADS:
                 quantise_wv(s // 2)
             if is_head(s + 1):
-                for bank_name, blocks in SCORE_BANKS:
-                    scores(s + 1, bank_name, blocks)
+                for bank in SCORE_BANKS[:2]:
+                    scores(s + 1, *bank)
+            wv_head = s // 2 + 1 if s % 2 == 0 and 0 <= s < 2 * (HEADS - 1) else None
+            if wv_head in (1, 2):
+                transpose_wv(wv_head, ps_misc, "o")
+                copy_wv(wv_head)
+            elif wv_head:
+                transpose_wv(wv_head, ps_scores, SCORE_BANKS[2][0])
+                copy_wv(wv_head)
+            if is_head(s + 1) and wv_head in (None, 1, 2):
+                scores(s + 1, *SCORE_BANKS[2])
             if s == len(heads) - 1:
                 project_v(s)
-            if is_head(s - 1):
-                spread_rinv(s - 1)
-                copy_rinv(s - 1)
             if is_head(s):
                 for i in BLOCK_ORDER:
                     transpose_e(s, i)
             if is_head(s):
                 copy_e(s, 2)
                 copy_e(s, 0)
+            if is_head(s - 1):
+                if takes_short_way(s - 1):
+                    spread_rinv(s - 1)
+                    copy_rinv(s - 1)
+                else:
+                    transpose_rinv(s - 1)
+                    park_rinv(s - 1)
             if s == 2:
                 spread_bias(1)
             if is_head(s - 1):
@@ -444,8 +505,9 @@ def tile_tatt_pa_kernel(tc, x, tem_embedding, Wv, bv, q, k, out):
                 unit, half = divmod(STEPS_OF_BATCH_1_XIN.index(s), 2)
                 for quarter in range(half * 2, half * 2 + 2):
                     regroup_xin_quarter(s, 1, *divmod(unit, PASSES), *divmod(quarter, PAIR))
-            if is_head(s - 2) and not on_gpsimd(s - 2):
-                normalise(s - 2)
+            for r in multiplied_in(s - 1):
+                if not on_gpsimd(r):
+                    normalise(r)
             if s == 1:
                 quantise_xin(0, 1, 0)
                 quantise_xin(0, 1, 1)
@@ -454,14 +516,14 @@ def tile_tatt_pa_kernel(tc, x, tem_embedding, Wv, bv, q, k, out):
                     quantise_xin(1, *divmod(unit, PASSES))
             if is_head(s) and s < len(heads) - 1:
                 project_v(s)
-            if is_head(s - 1):
-                attend(s - 1)
+            for r in multiplied_in(s):
+                attend(r)
             if s == -1:
                 zero_masked_half()
                 spread_bias(0)
-                transpose_wv(0)
-            if s % 2 == 0 and s >= 0 and s // 2 + 1 < HEADS:
-                transpose_wv(s // 2 + 1)
+                transpose_wv(0, ps_misc, "r")
+            if wv_head not in (None, 1, 2):
+                scores(s + 1, *SCORE_BANKS[2])
 
         for s in range(-1, len(heads) + 2):
             one_step(s)

import math
from contextlib import ExitStack

import concourse.mybir as mybir
from concourse.masks import make_identity

F32 = mybir.dt.float32
BF16 = mybir.dt.bfloat16
U32 = mybir.dt.uint32
U8 = mybir.dt.uint8
FP8X4 = mybir.dt.float8_e4m3fn_x4
ALU = mybir.AluOpType
ACT = mybir.ActivationFunctionType

P = 128
PACK = 4
B, NODES, T, HEADS, DH = 2, 2, 512, 8, 128
CIN = 1024
PASSES = CIN // (P * PACK)
BLOCKS = T // P
COPIES = P // BLOCKS
PAIR = 2
HALVES = PACK // PAIR
SCALE = 1.0 / math.sqrt(DH)
MASK_ADDEND = -(2.0**19)

FLOPS = 2 * B * NODES * T * CIN * HEADS * DH + 2 * (2 * B * NODES * HEADS * T * T * DH)


SCORE_BANKS = (("bank_3", (3,)), ("bank_2_0", (2, 0)), ("bank_1", (1,)))
BLOCK_ORDER = (3, 2, 0, 1)
QUARTERS = 4
SHORT_WAY = 2
STEPS_OF_BATCH_1_XIN = [3, 4, 6, 7, 9, 10, 12, 13]
LOADED_AHEAD = 3


def tile_tatt_pa_kernel(tc, x, tem_embedding, Wv, bv, q, k, out):
    nc = tc.nc
    heads = [(b, h, n) for b in range(B) for h in range(HEADS) for n in range(NODES)]

    with ExitStack() as ctx:
        keep = ctx.enter_context(tc.tile_pool(name="keep", bufs=1))
        stage = ctx.enter_context(tc.tile_pool(name="stage", bufs=2))
        small = ctx.enter_context(tc.tile_pool(name="small", bufs=3))
        handoff = ctx.enter_context(tc.tile_pool(name="handoff", bufs=3))
        ps_scores = ctx.enter_context(tc.psum_pool(name="ps_scores", bufs=1))
        ps_et = ctx.enter_context(tc.psum_pool(name="ps_et", bufs=1))
        ps_misc = ctx.enter_context(tc.psum_pool(name="ps_misc", bufs=1))

        ctx.enter_context(tc.manual_schedule())

        q_all = keep.tile([P, B * HEADS, NODES * T], BF16)
        k_all = keep.tile([P, B * HEADS, NODES * T], BF16)
        wv_raw = keep.tile([P, HEADS, CIN], BF16)
        xin_raw = keep.tile([P, B, NODES, PASSES, PACK, T], BF16)
        bias_all = keep.tile([P, HEADS * DH], BF16)

        def load_qk(b, h):
            channels = slice(h * DH, (h + 1) * DH)
            nc.sync.dma_start(out=q_all[:, b * HEADS + h, :], in_=q[b, channels].rearrange("c n t -> c (n t)"))
            nc.sync.dma_start(out=k_all[:, b * HEADS + h, :], in_=k[b, channels].rearrange("c n t -> c (n t)"))

        def load_wv(h):
            channels = slice(h * DH, (h + 1) * DH)
            nc.sync.dma_start(out=wv_raw[:, h, :], in_=Wv[channels, :])

        def load_xin(b, n):
            for g, stream in enumerate((x, tem_embedding)):
                nc.sync.dma_start(
                    out=xin_raw[:, b, n, g],
                    in_=stream[b, :, n, :].rearrange("(p j) t -> p j t", j=PACK),
                )

        def load_qk_node(b, h, n):
            channels = slice(h * DH, (h + 1) * DH)
            steps = slice(n * T, (n + 1) * T)
            nc.sync.dma_start(out=q_all[:, b * HEADS + h, steps], in_=q[b, channels, n, :])
            nc.sync.dma_start(out=k_all[:, b * HEADS + h, steps], in_=k[b, channels, n, :])

        bias_rows = keep.tile([P, HEADS * DH], BF16)
        nc.vector.memset(bias_rows[:], 0.0)
        load_qk_node(0, 0, 0)
        nc.sync.dma_start(out=bias_rows[0:1, :], in_=bv.unsqueeze(0))
        load_xin(0, 0)
        load_wv(0)
        load_qk_node(0, 0, 1)
        load_xin(0, 1)
        for h in range(1, LOADED_AHEAD):
            load_wv(h)
            load_qk(0, h)

        def load_for_later(s):
            if s % 2 == 0 and 0 <= s // 2 + LOADED_AHEAD < HEADS and s >= 0:
                load_wv(s // 2 + LOADED_AHEAD)
                load_qk(0, s // 2 + LOADED_AHEAD)
            if s in (1, 3):
                load_xin(1, s // 2)
            if s % 2 == 1 and 0 <= (s - 5) // 2 < HEADS:
                load_qk(1, (s - 5) // 2)

        table_loader = keep.tile([P, 1], F32)
        nc.vector.memset(table_loader[:], 0.0)
        nc.scalar.activation(out=table_loader[:], in_=table_loader[:], func=ACT.Exp)
        mask_f32 = keep.tile([P, P], F32)
        nc.gpsimd.memset(mask_f32[:], 0.0)
        nc.gpsimd.affine_select(
            out=mask_f32[:],
            in_=mask_f32[:],
            compare_op=ALU.is_ge,
            fill=MASK_ADDEND,
            base=0,
            pattern=[[-1, P]],
            channel_multiplier=1,
        )
        mask_bf = keep.tile([P, P], BF16)
        nc.vector.tensor_copy(out=mask_bf[:], in_=mask_f32[:])
        ones_bf = keep.tile([P, P], BF16)
        nc.vector.memset(ones_bf[:], 1.0)
        ident_bf = keep.tile([P, P], BF16)
        make_identity(nc, ident_bf[:])
        ident_f32 = keep.tile([P, P], F32)
        make_identity(nc, ident_f32[:])

        e_buffers = [keep.tile([P, BLOCKS, T], BF16, name="e_rows%d" % r) for r in range(2)]
        for e_buffer in e_buffers:
            nc.vector.memset(e_buffer[:, 0, P:T], 0.0)
            nc.vector.memset(e_buffer[:, 2, 3 * P : T], 0.0)

        x_codes = keep.tile([P, B, PASSES, NODES * T], U32, align_bytes=64)
        x_scales = keep.tile([P, B, PASSES, NODES * T], U8, align_bytes=64)
        w_codes = keep.tile([P, HEADS, PASSES, DH], U32, align_bytes=64)
        w_scales = keep.tile([P, HEADS, PASSES, DH], U8, align_bytes=64)

        tiles = {}

        def grouped_view(b, n, g):
            if ("x_grouped", (b, n, g)) not in tiles:
                tiles["x_grouped", (b, n, g)] = stage.tile([P, T, PACK], BF16, align_bytes=64, name="x_grouped", bufs=4)
            ordered = tiles["x_grouped", (b, n, g)][:].rearrange("p (w r m) j -> p w r m j", w=HALVES, r=PAIR)
            given = xin_raw[:, b, n, g].rearrange("p j (w m r) -> p w r m j", w=HALVES, r=PAIR)
            return ordered, given

        def regroup_xin(b, n, g, copy):
            ordered, given = grouped_view(b, n, g)
            copy(out=ordered, in_=given)

        def give_way(s):
            one = small.tile([P, 1], F32, name="one")
            nc.vector.memset(one[:], 1.0)
            tiles["one", s] = one

        def regroup_xin_quarter(s, b, n, g, w, r):
            ordered, given = grouped_view(b, n, g)
            nc.gpsimd.tensor_scalar(
                out=ordered[:, w, r],
                in0=given[:, w, r],
                scalar1=tiles["one", s][:],
                scalar2=0.0,
                op0=ALU.mult,
                op1=ALU.add,
            )

        def quantise_xin(b, n, g):
            steps = slice(n * T, (n + 1) * T)
            nc.vector.quantize_mx(
                out=x_codes[:, b, g, steps].bitcast(FP8X4),
                scales=x_scales[:, b, g, steps],
                in_=tiles.pop(("x_grouped", (b, n, g)))[:].rearrange("p t j -> p (t j)"),
            )

        def transpose_wv(h, pool, bank_name):
            words = wv_raw[:, h, :].bitcast(F32)
            words_per_pass = P * HALVES
            wt_ps = pool.tile([P, PASSES, HALVES, DH], F32, tag=bank_name)
            for g in range(PASSES):
                for half in range(HALVES):
                    nc.tensor.transpose(
                        wt_ps[:, g, half, :],
                        words[:, g * words_per_pass + half : (g + 1) * words_per_pass : HALVES],
                        ident_f32[:],
                    )
            tiles["wt_ps", h] = wt_ps

        def copy_wv(h):
            w_grouped = stage.tile([P, PASSES * DH * PACK], BF16, align_bytes=64)
            tiles["w_grouped", h] = w_grouped
            nc.scalar.copy(
                out=w_grouped[:].bitcast(F32).rearrange("p (g o half) -> p g o half", g=PASSES, half=HALVES),
                in_=tiles.pop(("wt_ps", h))[:].rearrange("p g half o -> p g o half"),
            )

        def quantise_wv(h):
            nc.vector.quantize_mx(
                out=w_codes[:, h].rearrange("p g o -> p (g o)").bitcast(FP8X4),
                scales=w_scales[:, h].rearrange("p g o -> p (g o)"),
                in_=tiles.pop(("w_grouped", h))[:],
            )

        def scores(s, bank_name, blocks):
            b, h, n = heads[s]
            q_head = q_all[:, b * HEADS + h, n * T : (n + 1) * T]
            k_head = k_all[:, b * HEADS + h, n * T : (n + 1) * T]
            bank = ps_scores.tile([P, T], F32, tag=bank_name)
            first_column = 0
            for i in blocks:
                width = (i + 1) * P
                s_ps = bank[:, first_column : first_column + width]
                first_column += width
                nc.tensor.matmul(
                    out=s_ps, lhsT=q_head[:, i * P : (i + 1) * P], rhs=k_head[:, 0:width], start=True, stop=False
                )
                nc.tensor.matmul(
                    out=s_ps[:, i * P : width], lhsT=ident_bf[:], rhs=mask_bf[:], start=False, stop=True
                )
                tiles["s_ps", (s, i)] = s_ps

        def open_softmax(s):
            tiles["negated", s] = stage.tile([P, BLOCKS, T], F32, name="negated")
            tiles["shift", s] = small.tile([P, BLOCKS], F32, name="shift")
            tiles["rowsum", s] = small.tile([P, BLOCKS], F32, name="rowsum")

        def rowmax(s, i):
            nc.vector.tensor_scalar(
                out=tiles["negated", s][:, i, 0 : (i + 1) * P],
                in0=tiles.pop(("s_ps", (s, i))),
                scalar1=-SCALE,
                scalar2=None,
                op0=ALU.mult,
                op1=ALU.min,
                accum_out=tiles["shift", s][:, i : i + 1],
            )

        def exp_block(s, i):
            width = (i + 1) * P
            nc.scalar.activation(
                out=e_buffers[s % len(e_buffers)][:, i, 0:width],
                in_=tiles["negated", s][:, i, 0:width],
                func=ACT.Exp,
                bias=tiles["shift", s][:, i : i + 1],
                scale=-1.0,
                accum_out=tiles["rowsum", s][:, i : i + 1],
            )

        def reciprocal_rowsum(s):
            rinv = small.tile([P, BLOCKS], F32, name="rinv")
            nc.vector.reciprocal(out=rinv[:], in_=tiles.pop(("rowsum", s))[:])
            tiles["rinv", s] = rinv

        def copies_in_hbm(s):
            b, h, n = heads[s // 2 * 2 + 2]
            first = h * DH + s % 2 * (DH // 2)
            return out[b, first : first + DH // 2].rearrange("c n t -> (c n t)")

        def repeat_rinv(s):
            rinv_copies = small.tile([P, COPIES, BLOCKS], F32, name="rinv_copies")
            nc.gpsimd.tensor_scalar(
                out=rinv_copies[:],
                in0=tiles.pop(("rinv", s))[:].unsqueeze(1).to_broadcast([P, COPIES, BLOCKS]),
                scalar1=1.0,
                scalar2=0.0,
                op0=ALU.mult,
                op1=ALU.add,
            )
            tiles["rinv_copies", s] = rinv_copies

        def transpose_rinv(s):
            r_ps = ps_misc.tile([P, T], F32, tag="r")
            copies = tiles.pop(("rinv_copies", s))
            nc.tensor.transpose(r_ps[:, 0:P], copies[:].rearrange("p k i -> p (k i)"), ident_f32[:])
            tiles["r_ps", s] = r_ps

        def park_rinv(s):
            r_rows = handoff.tile([P, P], F32, name="r_rows")
            nc.scalar.copy(out=r_rows[:], in_=tiles.pop(("r_ps", s))[:, 0:P])
            nc.sync.dma_start(
                out=copies_in_hbm(s).rearrange("(c p t) -> p c t", c=BLOCKS, p=P),
                in_=r_rows[:].unsqueeze(1).to_broadcast([P, BLOCKS, P]),
            )

        def fetch_rinv(s):
            r_sb = handoff.tile([P, T], F32, name="r_sb", bufs=4)
            nc.sync.dma_start(out=r_sb[:], in_=copies_in_hbm(s).rearrange("(p t) -> p t", p=P))
            tiles["r_sb", s] = r_sb

        def spread_rinv(s):
            rinv = tiles.pop(("rinv", s))
            r_ps = ps_misc.tile([P, T], F32, tag="r")
            for i in range(BLOCKS):
                nc.tensor.transpose(r_ps[:, i * P : (i + 1) * P], rinv[:, i : i + 1].to_broadcast([P, P]), ident_f32[:])
            tiles["r_ps", s] = r_ps

        def copy_rinv(s):
            r_sb = handoff.tile([P, T], F32, name="r_sb", bufs=4)
            nc.scalar.copy(out=r_sb[:], in_=tiles.pop(("r_ps", s))[:])
            tiles["r_sb", s] = r_sb

        et_banks = {
            0: ps_et.tile([P, 2, HALVES, P], F32, name="et_blocks_0_1"),
            2: ps_et.tile([P, 2, HALVES, P], F32, name="et_blocks_2_3"),
        }

        def spread_bias(half):
            columns = slice(half * T, (half + 1) * T)
            bias_ps = ps_misc.tile([P, T], F32, tag="r")
            nc.tensor.matmul(out=bias_ps[:], lhsT=ones_bf[:], rhs=bias_rows[:, columns], start=True, stop=True)
            nc.scalar.copy(out=bias_all[:, columns], in_=bias_ps[:])

        def zero_masked_half():
            zero_words = e_buffers[0][:, 0, T // 2 : T].bitcast(F32)
            for i in range(2):
                nc.tensor.transpose(et_banks[0][:, i, 1, :], zero_words, ident_f32[:])

        def transpose_e(s, i):
            first = i // 2 * 2
            e_words = e_buffers[s % len(e_buffers)][:, i, :].bitcast(F32)
            for w in range(i // 2 + 1):
                nc.tensor.transpose(
                    et_banks[first][:, i - first, w, :], e_words[:, w * P : (w + 1) * P], ident_f32[:]
                )

        def copy_e(s, first):
            if first == 2:
                tiles["e_grouped", s] = stage.tile([P, T * PACK], BF16, align_bytes=64, name="e_grouped")
            words = tiles["e_grouped", s][:].bitcast(F32).rearrange("p (i t w) -> p i t w", i=BLOCKS, w=HALVES)
            nc.scalar.copy(
                out=words[:, first : first + 2],
                in_=et_banks[first][:].rearrange("p i w t -> p i t w"),
            )

        def quantise_e(s):
            e_codes = handoff.tile([P, T], U32, align_bytes=64)
            e_scales = handoff.tile([P, T], U8, align_bytes=64)
            nc.vector.quantize_mx(
                out=e_codes[:].bitcast(FP8X4), scales=e_scales[:], in_=tiles.pop(("e_grouped", s))[:]
            )
            tiles["e_mx", s] = (e_codes, e_scales)

        def project_v(s):
            b, h, n = heads[s]
            if s == len(heads) - 1:
                v_ps = ps_scores.tile([P, PACK, DH], F32, tag="bank_3")
            else:
                v_ps = ps_misc.tile([P, PACK, DH], F32, tag="v")
            for j in range(PACK):
                steps = slice(n * T + j * P, n * T + (j + 1) * P)
                for g in range(PASSES):
                    nc.tensor.matmul_mx(
                        out=v_ps[:, j, :],
                        lhsT=x_codes[:, b, g, steps].bitcast(FP8X4),
                        lhsT_scale=x_scales[:, b, g, steps],
                        rhs=w_codes[:, h, g, :].bitcast(FP8X4),
                        rhs_scale=w_scales[:, h, g, :],
                        start=(g == 0),
                        stop=(g == PASSES - 1),
                    )
            tiles["v_ps", s] = v_ps

        def add_bias(s):
            b, h, n = heads[s]
            v_grouped = stage.tile([P, DH, PACK], BF16, align_bytes=64)
            nc.vector.tensor_tensor(
                out=v_grouped[:],
                in0=tiles.pop(("v_ps", s))[:].rearrange("p j c -> p c j"),
                in1=bias_all[:, h * DH : (h + 1) * DH].unsqueeze(2).to_broadcast([P, DH, PACK]),
                op=ALU.add,
            )
            tiles["v_grouped", s] = v_grouped

        def quantise_v(s):
            v_codes = handoff.tile([P, DH], U32, align_bytes=64)
            v_scales = handoff.tile([P, DH], U8, align_bytes=64)
            nc.vector.quantize_mx(
                out=v_codes[:].bitcast(FP8X4),
                scales=v_scales[:],
                in_=tiles.pop(("v_grouped", s))[:].rearrange("p c j -> p (c j)"),
            )
            tiles["v_mx", s] = (v_codes, v_scales)

        def attend(s):
            e_codes, e_scales = tiles.pop(("e_mx", s))
            v_codes, v_scales = tiles.pop(("v_mx", s))
            o_bank = {len(heads) - 2: "bank_2_0", len(heads) - 1: "bank_1"}.get(s)
            if o_bank:
                o_ps = ps_scores.tile([P, T], F32, tag=o_bank)
            else:
                o_ps = ps_misc.tile([P, T], F32, tag="o")
            nc.tensor.matmul_mx(
                out=o_ps[:],
                lhsT=v_codes[:].bitcast(FP8X4),
                lhsT_scale=v_scales[:],
                rhs=e_codes[:].bitcast(FP8X4),
                rhs_scale=e_scales[:],
                start=True,
                stop=True,
            )
            tiles["o_ps", s] = o_ps

        def normalise(s):
            b, h, n = heads[s]
            o_sb = handoff.tile([P, T], F32, name="o_sb", bufs=4)
            nc.vector.tensor_tensor(
                out=o_sb[:], in0=tiles.pop(("o_ps", s))[:], in1=tiles.pop(("r_sb", s))[:], op=ALU.mult
            )
            nc.sync.dma_start(out=out[b, h * DH : (h + 1) * DH, n, :], in_=o_sb[:])

        def on_gpsimd(s):
            return (s % 3 == 1 or (s % 3 == 2 and s >= 11)) and s < 27

        def bring_product(s):
            o_raw = handoff.tile([P, T], F32, name="o_raw", bufs=2)
            nc.scalar.copy(out=o_raw[:], in_=tiles.pop(("o_ps", s))[:])
            tiles["o_raw", s] = o_raw

        def normalise_on_gpsimd(s):
            b, h, n = heads[s]
            o_sb = handoff.tile([P, T], F32, name="o_sb", bufs=4)
            o_raw = tiles.pop(("o_raw", s))
            r_sb = tiles.pop(("r_sb", s))
            for i in range(BLOCKS):
                piece = slice(i * P, (i + 1) * P)
                nc.gpsimd.tensor_tensor(out=o_sb[:, piece], in0=o_raw[:, piece], in1=r_sb[:, piece], op=ALU.mult)
            nc.sync.dma_start(out=out[b, h * DH : (h + 1) * DH, n, :], in_=o_sb[:])

        def takes_short_way(s):
            return s >= len(heads) - SHORT_WAY

        def multiplied_in(s):
            long_way = [s - 3] if 0 <= s - 3 < len(heads) - SHORT_WAY else []
            short_way = [s - 1] if is_head(s - 1) and takes_short_way(s - 1) else []
            return short_way + long_way

        def is_head(s):
            return 0 <= s < len(heads)

        def one_step(s):
            if 0 <= s - 3 and not takes_short_way(s - 3):
                fetch_rinv(s - 3)
            load_for_later(s)
            if s == 1:
                give_way(s)
                for quarter in range(QUARTERS):
                    regroup_xin_quarter(s, 0, 1, 1, *divmod(quarter, PAIR))
            if is_head(s):
                open_softmax(s)
                for i in BLOCK_ORDER:
                    rowmax(s, i)
            if is_head(s - 1):
                reciprocal_rowsum(s - 1)
                if not takes_short_way(s - 1):
                    repeat_rinv(s - 1)
            if s == 0:
                regroup_xin(0, 0, 0, nc.vector.tensor_copy)
                regroup_xin(0, 0, 1, nc.scalar.copy)
                copy_wv(0)
                regroup_xin(0, 1, 0, nc.vector.tensor_copy)
                quantise_xin(0, 0, 0)
                quantise_xin(0, 0, 1)
                quantise_wv(0)
            if is_head(s):
                for i in BLOCK_ORDER:
                    exp_block(s, i)
            for r in multiplied_in(s - 1):
                if on_gpsimd(r):
                    bring_product(r)
                    normalise_on_gpsimd(r)
            if is_head(s - 1):
                add_bias(s - 1)
            if s % 2 == 0 and 0 < s // 2 < HEADS:
                quantise_wv(s // 2)
            if is_head(s + 1):
                for bank in SCORE_BANKS[:2]:
                    scores(s + 1, *bank)
            wv_head = s // 2 + 1 if s % 2 == 0 and 0 <= s < 2 * (HEADS - 1) else None
            if wv_head in (1, 2):
                transpose_wv(wv_head, ps_misc, "o")
                copy_wv(wv_head)
            elif wv_head:
                transpose_wv(wv_head, ps_scores, SCORE_BANKS[2][0])
                copy_wv(wv_head)
            if is_head(s + 1) and wv_head in (None, 1, 2):
                scores(s + 1, *SCORE_BANKS[2])
            if s == len(heads) - 1:
                project_v(s)
            if is_head(s):
                for i in BLOCK_ORDER:
                    transpose_e(s, i)
            if is_head(s):
                copy_e(s, 2)
                copy_e(s, 0)
            if is_head(s - 1):
                if takes_short_way(s - 1):
                    spread_rinv(s - 1)
                    copy_rinv(s - 1)
                else:
                    transpose_rinv(s - 1)
                    park_rinv(s - 1)
            if s == 2:
                spread_bias(1)
            if is_head(s - 1):
                quantise_e(s - 1)
                quantise_v(s - 1)
            if s in STEPS_OF_BATCH_1_XIN:
                give_way(s)
                unit, half = divmod(STEPS_OF_BATCH_1_XIN.index(s), 2)
                for quarter in range(half * 2, half * 2 + 2):
                    regroup_xin_quarter(s, 1, *divmod(unit, PASSES), *divmod(quarter, PAIR))
            for r in multiplied_in(s - 1):
                if not on_gpsimd(r):
                    normalise(r)
            if s == 1:
                quantise_xin(0, 1, 0)
                quantise_xin(0, 1, 1)
            for unit in range(NODES * PASSES):
                if s == STEPS_OF_BATCH_1_XIN[unit * 2 + 1] + 1:
                    quantise_xin(1, *divmod(unit, PASSES))
            if is_head(s) and s < len(heads) - 1:
                project_v(s)
            for r in multiplied_in(s):
                attend(r)
            if s == -1:
                zero_masked_half()
                spread_bias(0)
                transpose_wv(0, ps_misc, "r")
            if wv_head not in (None, 1, 2):
                scores(s + 1, *SCORE_BANKS[2])

        for s in range(-1, len(heads) + 2):
            one_step(s)
